import numpy as np
import ml_dtypes


def mxq(x, axis, fmt="e4m3"):
    dtype, down = {"e4m3": (ml_dtypes.float8_e4m3fn, 7), "e5m2": (ml_dtypes.float8_e5m2, 14)}[fmt]
    v = np.moveaxis(np.asarray(x, np.float32).astype(ml_dtypes.bfloat16).astype(np.float64), axis, -1)
    blocks = v.reshape(v.shape[:-1] + (-1, 32))
    amax = np.abs(blocks).max(-1, keepdims=True)
    byte = np.maximum(np.where(amax > 0, np.frexp(amax)[1] - 1 + 127, 0) - down, 1)
    scale = np.exp2(byte - 127.0)
    codes = (blocks / scale).astype(np.float32).astype(dtype).astype(np.float64)
    return np.moveaxis((codes * scale).reshape(v.shape), -1, axis)


WIDE = False


def mx_kscale(k):
    if not WIDE:
        return np.ones(k)
    levels = np.array([10, -10, 5, -5, 0])
    a = np.random.permutation(np.resize(levels, k // 512 * 4)).reshape(k // 512, 4)
    idx = np.arange(k)
    return np.exp2(a[idx // 512, idx % 128 // 32])


BF16 = ml_dtypes.bfloat16


def bf(x):
    return np.asarray(x, np.float32).astype(BF16)


def f64(x):
    return np.asarray(x).astype(np.float64)


E2M1 = np.array([0.0, 0.5, 1.0, 1.5, 2.0, 3.0, 4.0, 6.0, -0.0, -0.5, -1.0, -1.5, -2.0, -3.0, -4.0, -6.0])


def pack_weight(w, fmt):
    k, n = w.shape
    w = f64(bf(w)).reshape(k // 32, 32, n)
    amax = np.abs(w).max(1)
    if fmt == "e4m3":
        byte = np.frexp(amax)[1] - 1 + 127 - 7
    else:
        mant, ex = np.frexp(amax / 6.0)
        byte = np.where(mant > 0.5, ex, ex - 1) + 127
    byte = np.clip(np.where(amax > 0, byte, 1), 1, 254)
    scaled = (w * np.exp2(127.0 - byte)[:, None, :]).reshape(k, n).astype(np.float32)
    by_word = np.ascontiguousarray(scaled.reshape(k // 512, 128, 4, n).transpose(0, 1, 3, 2))
    if fmt == "e4m3":
        words = by_word.astype(ml_dtypes.float8_e4m3fn).view(np.uint8)
    else:
        c = by_word.astype(ml_dtypes.float4_e2m1fn).view(np.uint8) & 0xF
        words = c[..., 0::2] | (c[..., 1::2] << 4)
    return np.ascontiguousarray(words), np.ascontiguousarray(byte.astype(np.uint8).reshape(k // 512, 16, n))


def unpack_weight(words, scales, fmt):
    g, p, n, _ = words.shape
    if fmt == "e4m3":
        vals = np.ascontiguousarray(words).view(ml_dtypes.float8_e4m3fn).astype(np.float64)
    else:
        nib = np.empty((g, p, n, 4), np.uint8)
        nib[..., 0::2] = words & 0xF
        nib[..., 1::2] = words >> 4
        vals = E2M1[nib]
    vals = vals * np.repeat(np.exp2(scales.astype(np.float64) - 127.0), 8, axis=1)[..., None]
    return vals.transpose(0, 1, 3, 2).reshape(g * 512, n)


B, NB, DIM, R = 2048, 2, 1024, 2
INTER = DIM // R
EPS = 1e-5
FMT = "e4m3"


def sigmoid(v):
    return 1.0 / (1.0 + np.exp(-v))


def setup_inputs():
    u = mx_kscale(INTER)
    t = bf(np.random.standard_normal((B, NB, DIM)))
    W1 = np.random.standard_normal((NB, INTER, DIM)) / np.sqrt(NB * DIM)
    W1_words, W1_scales = pack_weight(np.ascontiguousarray(W1.swapaxes(1, 2)).reshape(-1, INTER), FMT)
    b1 = bf(0.3 * np.random.standard_normal((NB, INTER)))
    g1 = bf((1.0 + 0.2 * np.random.standard_normal((NB, INTER))) * u)
    beta1 = bf(0.3 * np.random.standard_normal((NB, INTER)) * u)
    m1 = bf(0.3 * np.random.standard_normal((NB, INTER)))
    v1 = bf(np.random.uniform(0.5, 1.5, (NB, INTER)))
    W2 = np.random.standard_normal((NB, DIM, INTER)) * 1.5 / np.sqrt(INTER) / u
    W2_words, W2_scales = pack_weight(np.ascontiguousarray(W2.swapaxes(1, 2)).reshape(-1, DIM), FMT)
    b2 = bf(0.3 * np.random.standard_normal((NB, DIM)))
    g2 = bf(1.0 + 0.2 * np.random.standard_normal((NB, DIM)))
    beta2 = bf(0.3 * np.random.standard_normal((NB, DIM)))
    m2 = bf(0.3 * np.random.standard_normal((NB, DIM)))
    v2 = bf(np.random.uniform(0.5, 1.5, (NB, DIM)))
    return {
        "t": t,
        "W1_words": W1_words,
        "W1_scales": W1_scales,
        "b1": b1,
        "g1": g1,
        "beta1": beta1,
        "m1": m1,
        "v1": v1,
        "W2_words": W2_words,
        "W2_scales": W2_scales,
        "b2": b2,
        "g2": g2,
        "beta2": beta2,
        "m2": m2,
        "v2": v2,
    }


def reference(t, W1_words, W1_scales, b1, g1, beta1, m1, v1, W2_words, W2_scales, b2, g2, beta2, m2, v2):
    t = f64(t)
    s = t.sum(axis=1)
    a = mxq(s, 1, "e4m3") @ unpack_weight(W1_words, W1_scales, FMT).reshape(NB, DIM, INTER)
    h = a.transpose(1, 0, 2) + f64(b1)
    h = (h - f64(m1)) * (1.0 / np.sqrt(f64(v1) + EPS)) * f64(g1) + f64(beta1)
    h = np.maximum(h, 0.0)
    c = mxq(h, 2, "e4m3").transpose(1, 0, 2) @ unpack_weight(W2_words, W2_scales, FMT).reshape(NB, INTER, DIM)
    y = c.transpose(1, 0, 2) + f64(b2)
    y = (y - f64(m2)) * (1.0 / np.sqrt(f64(v2) + EPS)) * f64(g2) + f64(beta2)
    w = sigmoid(y)
    return (w * t).sum(axis=1) * 3.0

@@ -1,0 +1,282 @@
+from contextlib import ExitStack
+
+import concourse.masks as masks
+import concourse.mybir as mybir
+
+F32 = mybir.dt.float32
+BF16 = mybir.dt.bfloat16
+I32 = mybir.dt.int32
+U32 = mybir.dt.uint32
+U8 = mybir.dt.uint8
+FP8X4 = mybir.dt.float8_e4m3fn_x4
+ACT = mybir.ActivationFunctionType
+ALU = mybir.AluOpType
+
+P = 128
+PACK = 4
+K_PASS = P * PACK
+BATCH = 2048
+BRANCHES = 2
+DIM = 1024
+INTER = 512
+EPS = 1e-5
+
+GROUP = 512
+ROW_TILES = GROUP // P
+GROUPS = BATCH // GROUP
+HALVES = GROUPS * BRANCHES
+PIECES = GROUPS * 2
+PAIR = 2 * P
+S_PASSES = DIM // K_PASS
+CH1 = BRANCHES * INTER // P
+CH2 = BRANCHES * DIM // P
+CH = CH1 + CH2
+D_TILES = DIM // P
+D_PART = D_TILES // 2
+
+FLOPS = 2 * BATCH * BRANCHES * (DIM * INTER + INTER * DIM)
+
+
+def tile_af_2_pa_t_e_kernel(
+    tc, t, W1_words, W1_scales, b1, g1, beta1, m1, v1, W2_words, W2_scales, b2, g2, beta2, m2, v2, out
+):
+    nc = tc.nc
+    with ExitStack() as ctx:
+        const = ctx.enter_context(tc.tile_pool(name="const", bufs=1))
+        inputs = ctx.enter_context(tc.tile_pool(name="inputs", bufs=1))
+        work = ctx.enter_context(tc.tile_pool(name="work", bufs=2))
+        gates = ctx.enter_context(tc.tile_pool(name="gates", bufs=2 * D_PART))
+        terms = ctx.enter_context(tc.tile_pool(name="terms", bufs=D_PART))
+        sums = ctx.enter_context(tc.psum_pool(name="sums", bufs=4))
+        flips = ctx.enter_context(tc.psum_pool(name="flips", bufs=4))
+        ctx.enter_context(tc.manual_schedule())
+
+        t_rows = t.rearrange("(g r a) n d -> g r a n d", g=GROUPS, a=ROW_TILES)
+        out_rows = out.rearrange("(g r a) d -> g r a d", g=GROUPS, a=ROW_TILES)
+        t_sb = [inputs.tile([P, ROW_TILES, BRANCHES, DIM], BF16, name="t_sb%d" % g) for g in range(GROUPS)]
+
+        def load_t(g):
+            for pair in range(2):
+                tiles = slice(2 * pair, 2 * pair + 2)
+                nc.sync.dma_start(out=t_sb[g][:, tiles], in_=t_rows[g][:, tiles])
+
+        w1_codes = const.tile([P, BRANCHES * S_PASSES, INTER], U32, align_bytes=64)
+        w1_planes = const.tile([P, INTER], U8, align_bytes=64)
+        w2_codes = const.tile([P, BRANCHES, DIM], U32, align_bytes=64)
+        w2_planes = const.tile([P, DIM], U8, align_bytes=64)
+        nc.vector.memset(w1_planes[:].bitcast(I32), 0)
+        nc.vector.memset(w2_planes[:].bitcast(I32), 0)
+
+        def load_weight(codes, planes, words, scales):
+            passes = words.shape[0]
+            for quadrant in range(4):
+                nc.sync.dma_start(
+                    out=planes[32 * quadrant : 32 * quadrant + 4 * passes, :].bitcast(I32),
+                    in_=scales[:, 4 * quadrant : 4 * quadrant + 4, :].bitcast(I32),
+                )
+            for c in range(passes):
+                nc.sync.dma_start(
+                    out=codes[:, c, :].bitcast(I32),
+                    in_=words[c].rearrange("p n k -> p (n k)").bitcast(I32),
+                )
+
+        load_t(0)
+        load_weight(w1_codes, w1_planes, W1_words, W1_scales)
+        load_weight(w2_codes, w2_planes, W2_words, W2_scales)
+        for g in range(1, GROUPS):
+            load_t(g)
+
+        ident_bf = const.tile([P, P], BF16)
+        ident_f = const.tile([P, P], F32)
+        masks.make_identity(nc, ident_bf[:])
+        masks.make_identity(nc, ident_f[:])
+        vec_rows = const.tile([P, P], BF16)
+        nc.vector.memset(vec_rows[:], 0.0)
+        for v, (x1, x2) in enumerate(((b1, b2), (g1, g2), (beta1, beta2), (m1, m2), (v1, v2))):
+            nc.scalar.dma_start(out=vec_rows[CH * v : CH * v + CH1, :], in_=x1.rearrange("n (j m) -> (n j) m", m=P))
+            nc.scalar.dma_start(out=vec_rows[CH * v + CH1 : CH * (v + 1), :], in_=x2.rearrange("n (j m) -> (n j) m", m=P))
+        vec_ps = flips.tile([P, P], BF16, tag="flip")
+        nc.tensor.transpose(vec_ps[:], vec_rows[:], ident_bf[:])
+        vec = const.tile([P, P], F32)
+        nc.vector.tensor_copy(out=vec[:], in_=vec_ps[:])
+        bias_v, gain_v, beta_v, mean_v, var_v = [vec[:, CH * v : CH * (v + 1)] for v in range(5)]
+        factor = const.tile([P, CH], F32)
+        offset = const.tile([P, CH], F32)
+        nc.vector.tensor_scalar_add(factor[:], var_v, EPS)
+        nc.scalar.sqrt(factor[:], factor[:])
+        nc.vector.reciprocal(factor[:], factor[:])
+        nc.vector.tensor_mul(factor[:], factor[:], gain_v)
+        nc.vector.tensor_sub(offset[:], bias_v, mean_v)
+        nc.vector.tensor_mul(offset[:], offset[:], factor[:])
+        nc.vector.tensor_add(offset[:], offset[:], beta_v)
+
+        def as_words(tile3):
+            return tile3.rearrange("p x y -> p (x y)").bitcast(F32)
+
+        def interleave(grouped_words, bank, engine_copy):
+            engine_copy(out=grouped_words, in_=bank.rearrange("p u c -> p c u"))
+
+        s_rows, s_codes, s_planes = {}, {}, {}
+        h_cols, h_rows, h_codes, h_planes = {}, {}, {}, {}
+        gate_cols, out_sb = {}, {}
+
+        def add_branches(piece):
+            g, pair = divmod(piece, 2)
+            tiles = slice(2 * pair, 2 * pair + 2)
+            s_pair = work.tile([P, 2, DIM], BF16)
+            nc.vector.tensor_tensor(out=s_pair[:], in0=t_sb[g][:, tiles, 0, :], in1=t_sb[g][:, tiles, 1, :], op=ALU.add)
+            s_rows[piece] = s_pair
+
+        def quantise_sum(piece):
+            g, pair = divmod(piece, 2)
+            if pair == 0:
+                s_codes[g] = work.tile([P, S_PASSES, GROUP], U32, align_bytes=64, name="s_codes", tag="s_codes")
+                s_planes[g] = work.tile([P, S_PASSES, GROUP], U8, align_bytes=64, name="s_planes", tag="s_planes")
+            words = as_words(s_rows[piece][:])
+            s_grouped = work.tile([P, S_PASSES, PAIR, PACK], BF16, align_bytes=64)
+            for c in range(S_PASSES):
+                bank = flips.tile([P, 2, PAIR], F32, tag="flip")
+                for a in range(2):
+                    first = (DIM // 2) * a + (K_PASS // 2) * c
+                    for u in range(2):
+                        nc.tensor.transpose(
+                            bank[:, u, P * a : P * (a + 1)], words[:, first + u : first + K_PASS // 2 : 2], ident_f[:]
+                        )
+                copy = nc.vector.tensor_copy if c % 2 == 0 else nc.scalar.copy
+                interleave(as_words(s_grouped[:, c]).rearrange("p (c u) -> p c u", u=2), bank[:], copy)
+            columns = slice(PAIR * pair, PAIR * (pair + 1))
+            for c in range(S_PASSES):
+                nc.vector.quantize_mx(
+                    out=s_codes[g][:, c, columns].bitcast(FP8X4),
+                    scales=s_planes[g][:, c, columns],
+                    in_=s_grouped[:, c].rearrange("p c k -> p (c k)"),
+                )
+
+        def first_layer(half):
+            g, n = divmod(half, BRANCHES)
+            h_half = work.tile([P, INTER // P, GROUP], BF16)
+            for j in range(INTER // P):
+                channels = slice(P * j, P * (j + 1))
+                acc = sums.tile([P, GROUP], F32, tag="sum")
+                for c in range(S_PASSES):
+                    w = S_PASSES * n + c
+                    nc.tensor.matmul_mx(
+                        out=acc[:],
+                        lhsT=w1_codes[:, w, channels].bitcast(FP8X4),
+                        lhsT_scale=w1_planes[4 * w : P, channels],
+                        rhs=s_codes[g][:, c, :].bitcast(FP8X4),
+                        rhs_scale=s_planes[g][:, c, :],
+                        start=(c == 0),
+                        stop=(c == S_PASSES - 1),
+                    )
+                ch = (INTER // P) * n + j
+                nc.scalar.activation(
+                    out=h_half[:, j, :], in_=acc[:], func=ACT.Relu,
+                    bias=offset[:, ch : ch + 1], scale=factor[:, ch : ch + 1],
+                )
+            h_cols[half] = h_half
+
+        def hidden_to_rows(half):
+            sorted_rows = work.tile([P, ROW_TILES, INTER], BF16)
+            sorted_words = as_words(sorted_rows[:])
+            for pair in range(2):
+                bank = flips.tile([P, 2, INTER], BF16, tag="flip")
+                for a in range(2):
+                    rows = slice(P * (2 * pair + a), P * (2 * pair + a + 1))
+                    for j in range(INTER // P):
+                        nc.tensor.transpose(bank[:, a, P * j : P * (j + 1)], h_cols[half][:, j, rows], ident_bf[:])
+                nc.scalar.copy(
+                    out=sorted_words[:, INTER * pair : INTER * (pair + 1)].rearrange("r (a u p) -> r a u p", a=2, u=2),
+                    in_=as_words(bank[:]).rearrange("r (a p u) -> r a u p", a=2, u=2),
+                )
+            h_rows[half] = sorted_rows
+
+        def quantise_hidden(half):
+            sorted_words = as_words(h_rows[half][:])
+            h_grouped = work.tile([P, GROUP, PACK], BF16, align_bytes=64)
+            grouped_words = as_words(h_grouped[:]).rearrange("p (c u) -> p c u", u=2)
+            for pair in range(2):
+                bank = flips.tile([P, 2, PAIR], F32, tag="flip")
+                for a in range(2):
+                    for u in range(2):
+                        first = (INTER // 2) * (2 * pair + a) + P * u
+                        nc.tensor.transpose(bank[:, u, P * a : P * (a + 1)], sorted_words[:, first : first + P], ident_f[:])
+                interleave(grouped_words[:, PAIR * pair : PAIR * (pair + 1), :], bank[:], nc.vector.tensor_copy)
+            h_codes[half] = work.tile([P, GROUP], U32, align_bytes=64, name="h_codes", tag="h_codes")
+            h_planes[half] = work.tile([P, GROUP], U8, align_bytes=64, name="h_planes", tag="h_planes")
+            nc.vector.quantize_mx(
+                out=h_codes[half][:].bitcast(FP8X4),
+                scales=h_planes[half][:],
+                in_=h_grouped[:].rearrange("p c k -> p (c k)"),
+            )
+
+        def second_layer(half, part):
+            n = half % BRANCHES
+            for j in range(D_PART * part, D_PART * (part + 1)):
+                features = slice(P * j, P * (j + 1))
+                acc = sums.tile([P, GROUP], F32, tag="sum")
+                nc.tensor.matmul_mx(
+                    out=acc[:],
+                    lhsT=w2_codes[:, n, features].bitcast(FP8X4),
+                    lhsT_scale=w2_planes[4 * n : P, features],
+                    rhs=h_codes[half][:].bitcast(FP8X4),
+                    rhs_scale=h_planes[half][:],
+                    start=True,
+                    stop=True,
+                )
+                ch = CH1 + D_TILES * n + j
+                gate = gates.tile([P, GROUP], F32)
+                nc.scalar.activation(
+                    out=gate[:], in_=acc[:], func=ACT.Sigmoid,
+                    bias=offset[:, ch : ch + 1], scale=factor[:, ch : ch + 1],
+                )
+                gate_cols[j] = gate
+
+        def apply_gates(half, part):
+            g, n = divmod(half, BRANCHES)
+            if n == 0 and part == 0:
+                out_sb[g] = work.tile([P, ROW_TILES, DIM], F32, name="out_sb", tag="out_sb")
+            for j in range(D_PART * part, D_PART * (part + 1)):
+                features = slice(P * j, P * (j + 1))
+                bank = flips.tile([P, ROW_TILES, P], F32, tag="flip")
+                for a in range(ROW_TILES):
+                    nc.tensor.transpose(bank[:, a, :], gate_cols[j][:, P * a : P * (a + 1)], ident_f[:])
+                if n == 0:
+                    term = out_sb[g][:, :, features]
+                else:
+                    term_sb = terms.tile([P, ROW_TILES, P], F32)
+                    term = term_sb[:]
+                nc.vector.scalar_tensor_tensor(
+                    out=term, in0=bank[:], scalar=3.0, in1=t_sb[g][:, :, n, features], op0=ALU.mult, op1=ALU.mult
+                )
+                if n == 1:
+                    nc.gpsimd.tensor_tensor(out=out_sb[g][:, :, features], in0=out_sb[g][:, :, features], in1=term, op=ALU.add)
+            if n == 1:
+                done = slice(P * D_PART * part, P * D_PART * (part + 1))
+                nc.sync.dma_start(out=out_rows[g][:, :, done], in_=out_sb[g][:, :, done])
+
+        S_LEAD = 3
+
+        def is_half(half):
+            return 0 <= half < HALVES
+
+        for step in range(-S_LEAD, HALVES + 1):
+            gated, flipped, started, piece = step - 1, step, step + 1, step + S_LEAD
+            if is_half(gated):
+                second_layer(gated, 0)
+            if is_half(flipped):
+                hidden_to_rows(flipped)
+            if is_half(gated):
+                second_layer(gated, 1)
+            if is_half(flipped):
+                quantise_hidden(flipped)
+            if is_half(gated):
+                apply_gates(gated, 0)
+            if 0 <= piece < PIECES:
+                add_branches(piece)
+            if is_half(started):
+                first_layer(started)
+            if is_half(gated):
+                apply_gates(gated, 1)
+            if 0 <= piece < PIECES:
+                quantise_sum(piece)

@@ -91,10 +91,10 @@ def tile_af_2_pa_t_e_kernel(
         masks.make_identity(nc, ident_bf[:])
         masks.make_identity(nc, ident_f[:])
         vec_rows = const.tile([P, P], BF16)
-        nc.vector.memset(vec_rows[:], 0.0)
         for v, (x1, x2) in enumerate(((b1, b2), (g1, g2), (beta1, beta2), (m1, m2), (v1, v2))):
             nc.scalar.dma_start(out=vec_rows[CH * v : CH * v + CH1, :], in_=x1.rearrange("n (j m) -> (n j) m", m=P))
             nc.scalar.dma_start(out=vec_rows[CH * v + CH1 : CH * (v + 1), :], in_=x2.rearrange("n (j m) -> (n j) m", m=P))
+        nc.scalar.dma_start(out=vec_rows[5 * CH :, :], in_=b1.rearrange("n (j m) -> (n j) m", m=P))
         vec_ps = flips.tile([P, P], BF16, tag="flip")
         nc.tensor.transpose(vec_ps[:], vec_rows[:], ident_bf[:])
         vec = const.tile([P, P], F32)
@@ -113,11 +113,14 @@ def tile_af_2_pa_t_e_kernel(
         def as_words(tile3):
             return tile3.rearrange("p x y -> p (x y)").bitcast(F32)
 
-        def interleave(grouped_words, bank, engine_copy):
-            engine_copy(out=grouped_words, in_=bank.rearrange("p u c -> p c u"))
+        out_bf = out.bitcast(BF16)
 
-        s_rows, s_codes, s_planes = {}, {}, {}
-        h_cols, h_rows, h_codes, h_planes = {}, {}, {}, {}
+        def parking(half):
+            g, n = divmod(half, BRANCHES)
+            return out_bf[GROUP * g + P * n : GROUP * g + P * (n + 1), :]
+
+        s_rows, s_grouped, s_codes, s_planes = {}, {}, {}, {}
+        h_lines, h_codes, h_planes = {}, {}, {}
         gate_cols, out_sb = {}, {}
 
         def add_branches(piece):
@@ -127,13 +130,9 @@ def tile_af_2_pa_t_e_kernel(
             nc.vector.tensor_tensor(out=s_pair[:], in0=t_sb[g][:, tiles, 0, :], in1=t_sb[g][:, tiles, 1, :], op=ALU.add)
             s_rows[piece] = s_pair
 
-        def quantise_sum(piece):
-            g, pair = divmod(piece, 2)
-            if pair == 0:
-                s_codes[g] = work.tile([P, S_PASSES, GROUP], U32, align_bytes=64, name="s_codes", tag="s_codes")
-                s_planes[g] = work.tile([P, S_PASSES, GROUP], U8, align_bytes=64, name="s_planes", tag="s_planes")
+        def transpose_sum(piece):
             words = as_words(s_rows[piece][:])
-            s_grouped = work.tile([P, S_PASSES, PAIR, PACK], BF16, align_bytes=64)
+            grouped = work.tile([P, S_PASSES, PAIR, PACK], BF16, align_bytes=64)
             for c in range(S_PASSES):
                 bank = flips.tile([P, 2, PAIR], F32, tag="flip")
                 for a in range(2):
@@ -142,14 +141,22 @@ def tile_af_2_pa_t_e_kernel(
                         nc.tensor.transpose(
                             bank[:, u, P * a : P * (a + 1)], words[:, first + u : first + K_PASS // 2 : 2], ident_f[:]
                         )
-                copy = nc.vector.tensor_copy if c % 2 == 0 else nc.scalar.copy
-                interleave(as_words(s_grouped[:, c]).rearrange("p (c u) -> p c u", u=2), bank[:], copy)
+                nc.scalar.copy(
+                    out=as_words(grouped[:, c]).rearrange("p (c u) -> p c u", u=2), in_=bank[:].rearrange("p u c -> p c u")
+                )
+            s_grouped[piece] = grouped
+
+        def quantise_sum(piece):
+            g, pair = divmod(piece, 2)
+            if pair == 0:
+                s_codes[g] = work.tile([P, S_PASSES, GROUP], U32, align_bytes=64, name="s_codes", tag="s_codes")
+                s_planes[g] = work.tile([P, S_PASSES, GROUP], U8, align_bytes=64, name="s_planes", tag="s_planes")
             columns = slice(PAIR * pair, PAIR * (pair + 1))
             for c in range(S_PASSES):
                 nc.vector.quantize_mx(
                     out=s_codes[g][:, c, columns].bitcast(FP8X4),
                     scales=s_planes[g][:, c, columns],
-                    in_=s_grouped[:, c].rearrange("p c k -> p (c k)"),
+                    in_=s_grouped[piece][:, c].rearrange("p c k -> p (c k)"),
                 )
 
         def first_layer(half):
@@ -174,34 +181,19 @@ def tile_af_2_pa_t_e_kernel(
                     out=h_half[:, j, :], in_=acc[:], func=ACT.Relu,
                     bias=offset[:, ch : ch + 1], scale=factor[:, ch : ch + 1],
                 )
-            h_cols[half] = h_half
-
-        def hidden_to_rows(half):
-            sorted_rows = work.tile([P, ROW_TILES, INTER], BF16)
-            sorted_words = as_words(sorted_rows[:])
-            for pair in range(2):
-                bank = flips.tile([P, 2, INTER], BF16, tag="flip")
-                for a in range(2):
-                    rows = slice(P * (2 * pair + a), P * (2 * pair + a + 1))
-                    for j in range(INTER // P):
-                        nc.tensor.transpose(bank[:, a, P * j : P * (j + 1)], h_cols[half][:, j, rows], ident_bf[:])
-                nc.scalar.copy(
-                    out=sorted_words[:, INTER * pair : INTER * (pair + 1)].rearrange("r (a u p) -> r a u p", a=2, u=2),
-                    in_=as_words(bank[:]).rearrange("r (a p u) -> r a u p", a=2, u=2),
-                )
-            h_rows[half] = sorted_rows
+            nc.sync.dma_start(
+                out=parking(half).rearrange("r x -> (r x)").rearrange("(j m c) -> m j c", j=INTER // P, m=P), in_=h_half[:]
+            )
+            lines = work.tile([P, PACK, GROUP], BF16)
+            nc.sync.dma_start(out=lines[:], in_=parking(half).rearrange("p (k c) -> p k c", k=PACK))
+            h_lines[half] = lines
 
         def quantise_hidden(half):
-            sorted_words = as_words(h_rows[half][:])
             h_grouped = work.tile([P, GROUP, PACK], BF16, align_bytes=64)
-            grouped_words = as_words(h_grouped[:]).rearrange("p (c u) -> p c u", u=2)
-            for pair in range(2):
-                bank = flips.tile([P, 2, PAIR], F32, tag="flip")
-                for a in range(2):
-                    for u in range(2):
-                        first = (INTER // 2) * (2 * pair + a) + P * u
-                        nc.tensor.transpose(bank[:, u, P * a : P * (a + 1)], sorted_words[:, first : first + P], ident_f[:])
-                interleave(grouped_words[:, PAIR * pair : PAIR * (pair + 1), :], bank[:], nc.vector.tensor_copy)
+            nc.vector.tensor_copy(
+                out=h_grouped[:].rearrange("p (c i) k -> p c k i", i=4),
+                in_=h_lines[half][:].rearrange("p k (c i) -> p c k i", i=4),
+            )
             h_codes[half] = work.tile([P, GROUP], U32, align_bytes=64, name="h_codes", tag="h_codes")
             h_planes[half] = work.tile([P, GROUP], U8, align_bytes=64, name="h_planes", tag="h_planes")
             nc.vector.quantize_mx(
@@ -253,30 +245,28 @@ def tile_af_2_pa_t_e_kernel(
                     nc.gpsimd.tensor_tensor(out=out_sb[g][:, :, features], in0=out_sb[g][:, :, features], in1=term, op=ALU.add)
             if n == 1:
                 done = slice(P * D_PART * part, P * D_PART * (part + 1))
-                nc.sync.dma_start(out=out_rows[g][:, :, done], in_=out_sb[g][:, :, done])
+                nc.gpsimd.dma_start(out=out_rows[g][:, :, done], in_=out_sb[g][:, :, done])
 
-        S_LEAD = 3
+        S_LEAD = 2
 
         def is_half(half):
             return 0 <= half < HALVES
 
-        for step in range(-S_LEAD, HALVES + 1):
-            gated, flipped, started, piece = step - 1, step, step + 1, step + S_LEAD
-            if is_half(gated):
-                second_layer(gated, 0)
-            if is_half(flipped):
-                hidden_to_rows(flipped)
-            if is_half(gated):
-                second_layer(gated, 1)
-            if is_half(flipped):
-                quantise_hidden(flipped)
-            if is_half(gated):
-                apply_gates(gated, 0)
-            if 0 <= piece < PIECES:
-                add_branches(piece)
-            if is_half(started):
-                first_layer(started)
-            if is_half(gated):
-                apply_gates(gated, 1)
-            if 0 <= piece < PIECES:
-                quantise_sum(piece)
+        for step in range(-S_LEAD, HALVES + 3):
+            if 0 <= step + S_LEAD - 1 < PIECES:
+                quantise_sum(step + S_LEAD - 1)
+            if 0 <= step + S_LEAD < PIECES:
+                add_branches(step + S_LEAD)
+            if is_half(step - 2):
+                second_layer(step - 2, 0)
+            if is_half(step - 3):
+                apply_gates(step - 3, 1)
+            if is_half(step - 2):
+                second_layer(step - 2, 1)
+                apply_gates(step - 2, 0)
+            if is_half(step - 1):
+                quantise_hidden(step - 1)
+            if is_half(step):
+                first_layer(step)
+            if 0 <= step + S_LEAD < PIECES:
+                transpose_sum(step + S_LEAD)

@@ -32,7 +32,9 @@ CH1 = BRANCHES * INTER // P
 CH2 = BRANCHES * DIM // P
 CH = CH1 + CH2
 D_TILES = DIM // P
-D_PART = D_TILES // 2
+SLAB_TILES = 2
+GROUP_SLABS = D_TILES // SLAB_TILES
+SLABS = GROUPS * GROUP_SLABS
 
 FLOPS = 2 * BATCH * BRANCHES * (DIM * INTER + INTER * DIM)
 
@@ -45,8 +47,9 @@ def tile_af_2_pa_t_e_kernel(
         const = ctx.enter_context(tc.tile_pool(name="const", bufs=1))
         inputs = ctx.enter_context(tc.tile_pool(name="inputs", bufs=1))
         work = ctx.enter_context(tc.tile_pool(name="work", bufs=2))
-        gates = ctx.enter_context(tc.tile_pool(name="gates", bufs=2 * D_PART))
-        terms = ctx.enter_context(tc.tile_pool(name="terms", bufs=D_PART))
+        operands = ctx.enter_context(tc.tile_pool(name="operands", bufs=4))
+        gates = ctx.enter_context(tc.tile_pool(name="gates", bufs=2 * SLAB_TILES * BRANCHES))
+        terms = ctx.enter_context(tc.tile_pool(name="terms", bufs=4))
         sums = ctx.enter_context(tc.psum_pool(name="sums", bufs=4))
         flips = ctx.enter_context(tc.psum_pool(name="flips", bufs=4))
         ctx.enter_context(tc.manual_schedule())
@@ -60,41 +63,40 @@ def tile_af_2_pa_t_e_kernel(
                 tiles = slice(2 * pair, 2 * pair + 2)
                 nc.sync.dma_start(out=t_sb[g][:, tiles], in_=t_rows[g][:, tiles])
 
-        w1_codes = const.tile([P, BRANCHES * S_PASSES, INTER], U32, align_bytes=64)
-        w1_planes = const.tile([P, INTER], U8, align_bytes=64)
-        w2_codes = const.tile([P, BRANCHES, DIM], U32, align_bytes=64)
-        w2_planes = const.tile([P, DIM], U8, align_bytes=64)
-        nc.vector.memset(w1_planes[:].bitcast(I32), 0)
-        nc.vector.memset(w2_planes[:].bitcast(I32), 0)
-
-        def load_weight(codes, planes, words, scales):
-            passes = words.shape[0]
+        def load_weight(words, scales, name):
+            passes, columns = words.shape[0], words.shape[2]
+            codes = const.tile([P, passes, columns], U32, align_bytes=64, name=name + "_codes")
+            planes = const.tile([P, columns], U8, align_bytes=64, name=name + "_planes")
+            nc.vector.memset(planes[:].bitcast(I32), 0)
+            nc.sync.dma_start(out=codes[:].bitcast(I32), in_=words.rearrange("c p n k -> p c (n k)").bitcast(I32))
             for quadrant in range(4):
                 nc.sync.dma_start(
                     out=planes[32 * quadrant : 32 * quadrant + 4 * passes, :].bitcast(I32),
                     in_=scales[:, 4 * quadrant : 4 * quadrant + 4, :].bitcast(I32),
                 )
-            for c in range(passes):
-                nc.sync.dma_start(
-                    out=codes[:, c, :].bitcast(I32),
-                    in_=words[c].rearrange("p n k -> p (n k)").bitcast(I32),
-                )
-
-        load_t(0)
-        load_weight(w1_codes, w1_planes, W1_words, W1_scales)
-        load_weight(w2_codes, w2_planes, W2_words, W2_scales)
-        for g in range(1, GROUPS):
-            load_t(g)
+            return codes, planes
 
         ident_bf = const.tile([P, P], BF16)
         ident_f = const.tile([P, P], F32)
-        masks.make_identity(nc, ident_bf[:])
         masks.make_identity(nc, ident_f[:])
+        masks.make_identity(nc, ident_bf[:])
+
         vec_rows = const.tile([P, P], BF16)
-        for v, (x1, x2) in enumerate(((b1, b2), (g1, g2), (beta1, beta2), (m1, m2), (v1, v2))):
-            nc.scalar.dma_start(out=vec_rows[CH * v : CH * v + CH1, :], in_=x1.rearrange("n (j m) -> (n j) m", m=P))
-            nc.scalar.dma_start(out=vec_rows[CH * v + CH1 : CH * (v + 1), :], in_=x2.rearrange("n (j m) -> (n j) m", m=P))
-        nc.scalar.dma_start(out=vec_rows[5 * CH :, :], in_=b1.rearrange("n (j m) -> (n j) m", m=P))
+        nc.vector.memset(vec_rows[:], 0.0)
+
+        def load_vectors(layer1, layer2, first):
+            for v, (x1, x2) in enumerate(zip(layer1, layer2)):
+                row = CH * (first + v)
+                nc.scalar.dma_start(out=vec_rows[row : row + CH1, :], in_=x1.rearrange("n (j m) -> (n j) m", m=P))
+                nc.scalar.dma_start(out=vec_rows[row + CH1 : row + CH, :], in_=x2.rearrange("n (j m) -> (n j) m", m=P))
+
+        load_vectors((b1, g1, beta1), (b2, g2, beta2), 0)
+        load_t(0)
+        load_vectors((m1, v1), (m2, v2), 3)
+        w1_codes, w1_planes = load_weight(W1_words, W1_scales, "w1")
+        load_t(1)
+        w2_codes, w2_planes = load_weight(W2_words, W2_scales, "w2")
+
         vec_ps = flips.tile([P, P], BF16, tag="flip")
         nc.tensor.transpose(vec_ps[:], vec_rows[:], ident_bf[:])
         vec = const.tile([P, P], F32)
@@ -181,11 +183,13 @@ def tile_af_2_pa_t_e_kernel(
                     out=h_half[:, j, :], in_=acc[:], func=ACT.Relu,
                     bias=offset[:, ch : ch + 1], scale=factor[:, ch : ch + 1],
                 )
-            nc.sync.dma_start(
+            nc.scalar.dma_start(
                 out=parking(half).rearrange("r x -> (r x)").rearrange("(j m c) -> m j c", j=INTER // P, m=P), in_=h_half[:]
             )
+
+        def fetch_hidden(half):
             lines = work.tile([P, PACK, GROUP], BF16)
-            nc.sync.dma_start(out=lines[:], in_=parking(half).rearrange("p (k c) -> p k c", k=PACK))
+            nc.scalar.dma_start(out=lines[:], in_=parking(half).rearrange("p (k c) -> p k c", k=PACK))
             h_lines[half] = lines
 
         def quantise_hidden(half):
@@ -194,25 +198,29 @@ def tile_af_2_pa_t_e_kernel(
                 out=h_grouped[:].rearrange("p (c i) k -> p c k i", i=4),
                 in_=h_lines[half][:].rearrange("p k (c i) -> p c k i", i=4),
             )
-            h_codes[half] = work.tile([P, GROUP], U32, align_bytes=64, name="h_codes", tag="h_codes")
-            h_planes[half] = work.tile([P, GROUP], U8, align_bytes=64, name="h_planes", tag="h_planes")
+            h_codes[half] = operands.tile([P, GROUP], U32, align_bytes=64, name="h_codes", tag="h_codes")
+            h_planes[half] = operands.tile([P, GROUP], U8, align_bytes=64, name="h_planes", tag="h_planes")
             nc.vector.quantize_mx(
                 out=h_codes[half][:].bitcast(FP8X4),
                 scales=h_planes[half][:],
                 in_=h_grouped[:].rearrange("p c k -> p (c k)"),
             )
 
-        def second_layer(half, part):
-            n = half % BRANCHES
-            for j in range(D_PART * part, D_PART * (part + 1)):
+        def slab_tiles(slab):
+            g, q = divmod(slab, GROUP_SLABS)
+            return g, [(SLAB_TILES * q + i, n) for i in range(SLAB_TILES) for n in range(BRANCHES)]
+
+        def second_layer(slab):
+            g, tiles = slab_tiles(slab)
+            for j, n in tiles:
                 features = slice(P * j, P * (j + 1))
                 acc = sums.tile([P, GROUP], F32, tag="sum")
                 nc.tensor.matmul_mx(
                     out=acc[:],
                     lhsT=w2_codes[:, n, features].bitcast(FP8X4),
                     lhsT_scale=w2_planes[4 * n : P, features],
-                    rhs=h_codes[half][:].bitcast(FP8X4),
-                    rhs_scale=h_planes[half][:],
+                    rhs=h_codes[BRANCHES * g + n][:].bitcast(FP8X4),
+                    rhs_scale=h_planes[BRANCHES * g + n][:],
                     start=True,
                     stop=True,
                 )
@@ -222,17 +230,17 @@ def tile_af_2_pa_t_e_kernel(
                     out=gate[:], in_=acc[:], func=ACT.Sigmoid,
                     bias=offset[:, ch : ch + 1], scale=factor[:, ch : ch + 1],
                 )
-                gate_cols[j] = gate
+                gate_cols[(j, n)] = gate
 
-        def apply_gates(half, part):
-            g, n = divmod(half, BRANCHES)
-            if n == 0 and part == 0:
+        def apply_gates(slab):
+            g, tiles = slab_tiles(slab)
+            if slab % GROUP_SLABS == 0:
                 out_sb[g] = work.tile([P, ROW_TILES, DIM], F32, name="out_sb", tag="out_sb")
-            for j in range(D_PART * part, D_PART * (part + 1)):
+            for j, n in tiles:
                 features = slice(P * j, P * (j + 1))
                 bank = flips.tile([P, ROW_TILES, P], F32, tag="flip")
                 for a in range(ROW_TILES):
-                    nc.tensor.transpose(bank[:, a, :], gate_cols[j][:, P * a : P * (a + 1)], ident_f[:])
+                    nc.tensor.transpose(bank[:, a, :], gate_cols[(j, n)][:, P * a : P * (a + 1)], ident_f[:])
                 if n == 0:
                     term = out_sb[g][:, :, features]
                 else:
@@ -243,30 +251,39 @@ def tile_af_2_pa_t_e_kernel(
                 )
                 if n == 1:
                     nc.gpsimd.tensor_tensor(out=out_sb[g][:, :, features], in0=out_sb[g][:, :, features], in1=term, op=ALU.add)
-            if n == 1:
-                done = slice(P * D_PART * part, P * D_PART * (part + 1))
-                nc.gpsimd.dma_start(out=out_rows[g][:, :, done], in_=out_sb[g][:, :, done])
+            first = tiles[0][0]
+            done = slice(P * first, P * (first + SLAB_TILES))
+            nc.sync.dma_start(out=out_rows[g][:, :, done], in_=out_sb[g][:, :, done])
 
         S_LEAD = 2
+        GATE_LAG = 4
 
         def is_half(half):
             return 0 <= half < HALVES
 
-        for step in range(-S_LEAD, HALVES + 3):
+        def is_slab(slab):
+            return 0 <= slab < SLABS
+
+        for step in range(-S_LEAD, HALVES + GATE_LAG + 1):
+            slab = 2 * (step - GATE_LAG)
             if 0 <= step + S_LEAD - 1 < PIECES:
                 quantise_sum(step + S_LEAD - 1)
             if 0 <= step + S_LEAD < PIECES:
                 add_branches(step + S_LEAD)
+            if step in (0, 2):
+                load_t(2 + step // 2)
+            if is_slab(slab):
+                second_layer(slab)
+            if is_slab(slab - 1):
+                apply_gates(slab - 1)
             if is_half(step - 2):
-                second_layer(step - 2, 0)
-            if is_half(step - 3):
-                apply_gates(step - 3, 1)
-            if is_half(step - 2):
-                second_layer(step - 2, 1)
-                apply_gates(step - 2, 0)
-            if is_half(step - 1):
-                quantise_hidden(step - 1)
+                quantise_hidden(step - 2)
+            if is_slab(slab):
+                second_layer(slab + 1)
+                apply_gates(slab)
             if is_half(step):
                 first_layer(step)
+            if is_half(step - 1):
+                fetch_hidden(step - 1)
             if 0 <= step + S_LEAD < PIECES:
                 transpose_sum(step + S_LEAD)

@@ -58,10 +58,14 @@ def tile_af_2_pa_t_e_kernel(
         out_rows = out.rearrange("(g r a) d -> g r a d", g=GROUPS, a=ROW_TILES)
         t_sb = [inputs.tile([P, ROW_TILES, BRANCHES, DIM], BF16, name="t_sb%d" % g) for g in range(GROUPS)]
 
+        def load_piece(piece):
+            g, pair = divmod(piece, 2)
+            tiles = slice(2 * pair, 2 * pair + 2)
+            nc.sync.dma_start(out=t_sb[g][:, tiles], in_=t_rows[g][:, tiles])
+
         def load_t(g):
-            for pair in range(2):
-                tiles = slice(2 * pair, 2 * pair + 2)
-                nc.sync.dma_start(out=t_sb[g][:, tiles], in_=t_rows[g][:, tiles])
+            load_piece(2 * g)
+            load_piece(2 * g + 1)
 
         def load_weight(words, scales, name):
             passes, columns = words.shape[0], words.shape[2]
@@ -93,24 +97,28 @@ def tile_af_2_pa_t_e_kernel(
         load_vectors((b1, g1, beta1), (b2, g2, beta2), 0)
         load_t(0)
         load_vectors((m1, v1), (m2, v2), 3)
+        load_piece(2)
         w1_codes, w1_planes = load_weight(W1_words, W1_scales, "w1")
-        load_t(1)
+        load_piece(3)
+        load_t(2)
         w2_codes, w2_planes = load_weight(W2_words, W2_scales, "w2")
 
-        vec_ps = flips.tile([P, P], BF16, tag="flip")
-        nc.tensor.transpose(vec_ps[:], vec_rows[:], ident_bf[:])
-        vec = const.tile([P, P], F32)
-        nc.vector.tensor_copy(out=vec[:], in_=vec_ps[:])
-        bias_v, gain_v, beta_v, mean_v, var_v = [vec[:, CH * v : CH * (v + 1)] for v in range(5)]
         factor = const.tile([P, CH], F32)
         offset = const.tile([P, CH], F32)
-        nc.vector.tensor_scalar_add(factor[:], var_v, EPS)
-        nc.scalar.sqrt(factor[:], factor[:])
-        nc.vector.reciprocal(factor[:], factor[:])
-        nc.vector.tensor_mul(factor[:], factor[:], gain_v)
-        nc.vector.tensor_sub(offset[:], bias_v, mean_v)
-        nc.vector.tensor_mul(offset[:], offset[:], factor[:])
-        nc.vector.tensor_add(offset[:], offset[:], beta_v)
+
+        def channel_factors():
+            vec_ps = flips.tile([P, P], BF16, tag="flip")
+            nc.tensor.transpose(vec_ps[:], vec_rows[:], ident_bf[:])
+            vec = const.tile([P, P], F32)
+            nc.vector.tensor_copy(out=vec[:], in_=vec_ps[:])
+            bias_v, gain_v, beta_v, mean_v, var_v = [vec[:, CH * v : CH * (v + 1)] for v in range(5)]
+            nc.vector.tensor_scalar_add(factor[:], var_v, EPS)
+            nc.scalar.sqrt(factor[:], factor[:])
+            nc.vector.reciprocal(factor[:], factor[:])
+            nc.vector.tensor_mul(factor[:], factor[:], gain_v)
+            nc.vector.tensor_sub(offset[:], bias_v, mean_v)
+            nc.vector.tensor_mul(offset[:], offset[:], factor[:])
+            nc.vector.tensor_add(offset[:], offset[:], beta_v)
 
         def as_words(tile3):
             return tile3.rearrange("p x y -> p (x y)").bitcast(F32)
@@ -122,7 +130,7 @@ def tile_af_2_pa_t_e_kernel(
             return out_bf[GROUP * g + P * n : GROUP * g + P * (n + 1), :]
 
         s_rows, s_grouped, s_codes, s_planes = {}, {}, {}, {}
-        h_lines, h_codes, h_planes = {}, {}, {}
+        h_cols, h_lines, h_codes, h_planes = {}, {}, {}, {}
         gate_cols, out_sb = {}, {}
 
         def add_branches(piece):
@@ -183,13 +191,17 @@ def tile_af_2_pa_t_e_kernel(
                     out=h_half[:, j, :], in_=acc[:], func=ACT.Relu,
                     bias=offset[:, ch : ch + 1], scale=factor[:, ch : ch + 1],
                 )
+            h_cols[half] = h_half
+
+        def park_hidden(half):
+            h_half = h_cols[half]
             nc.scalar.dma_start(
                 out=parking(half).rearrange("r x -> (r x)").rearrange("(j m c) -> m j c", j=INTER // P, m=P), in_=h_half[:]
             )
 
         def fetch_hidden(half):
             lines = work.tile([P, PACK, GROUP], BF16)
-            nc.scalar.dma_start(out=lines[:], in_=parking(half).rearrange("p (k c) -> p k c", k=PACK))
+            nc.sync.dma_start(out=lines[:], in_=parking(half).rearrange("p (k c) -> p k c", k=PACK))
             h_lines[half] = lines
 
         def quantise_hidden(half):
@@ -251,6 +263,9 @@ def tile_af_2_pa_t_e_kernel(
                 )
                 if n == 1:
                     nc.gpsimd.tensor_tensor(out=out_sb[g][:, :, features], in0=out_sb[g][:, :, features], in1=term, op=ALU.add)
+
+        def store_slab(slab):
+            g, tiles = slab_tiles(slab)
             first = tiles[0][0]
             done = slice(P * first, P * (first + SLAB_TILES))
             nc.sync.dma_start(out=out_rows[g][:, :, done], in_=out_sb[g][:, :, done])
@@ -266,12 +281,12 @@ def tile_af_2_pa_t_e_kernel(
 
         for step in range(-S_LEAD, HALVES + GATE_LAG + 1):
             slab = 2 * (step - GATE_LAG)
-            if 0 <= step + S_LEAD - 1 < PIECES:
-                quantise_sum(step + S_LEAD - 1)
             if 0 <= step + S_LEAD < PIECES:
                 add_branches(step + S_LEAD)
-            if step in (0, 2):
-                load_t(2 + step // 2)
+            if step == -S_LEAD:
+                channel_factors()
+            if 0 <= step + S_LEAD - 1 < PIECES:
+                quantise_sum(step + S_LEAD - 1)
             if is_slab(slab):
                 second_layer(slab)
             if is_slab(slab - 1):
@@ -285,5 +300,13 @@ def tile_af_2_pa_t_e_kernel(
                 first_layer(step)
             if is_half(step - 1):
                 fetch_hidden(step - 1)
+            if is_half(step):
+                park_hidden(step)
+            if step == 2:
+                load_t(3)
+            if is_slab(slab - 1):
+                store_slab(slab - 1)
+            if is_slab(slab):
+                store_slab(slab)
             if 0 <= step + S_LEAD < PIECES:
                 transpose_sum(step + S_LEAD)

@@ -52,7 +52,6 @@ def tile_af_2_pa_t_e_kernel(
         terms = ctx.enter_context(tc.tile_pool(name="terms", bufs=4))
         sums = ctx.enter_context(tc.psum_pool(name="sums", bufs=4))
         flips = ctx.enter_context(tc.psum_pool(name="flips", bufs=4))
-        ctx.enter_context(tc.manual_schedule())
 
         t_rows = t.rearrange("(g r a) n d -> g r a n d", g=GROUPS, a=ROW_TILES)
         out_rows = out.rearrange("(g r a) d -> g r a d", g=GROUPS, a=ROW_TILES)

@@ -84,52 +84,74 @@ def tile_af_2_pa_t_e_kernel(
         masks.make_identity(nc, ident_f[:])
         masks.make_identity(nc, ident_bf[:])
 
-        vec_rows = const.tile([P, P], BF16)
-        nc.vector.memset(vec_rows[:], 0.0)
+        VEC_PAD = 16
+        vec1_bf = const.tile([P, 5, VEC_PAD], BF16)
+        vec2_rows = const.tile([P, P], BF16)
+        nc.vector.memset(vec2_rows[:], 0.0)
 
-        def load_vectors(layer1, layer2, first):
-            for v, (x1, x2) in enumerate(zip(layer1, layer2)):
-                row = CH * (first + v)
-                nc.scalar.dma_start(out=vec_rows[row : row + CH1, :], in_=x1.rearrange("n (j m) -> (n j) m", m=P))
-                nc.scalar.dma_start(out=vec_rows[row + CH1 : row + CH, :], in_=x2.rearrange("n (j m) -> (n j) m", m=P))
+        def load_vectors1(vectors):
+            for v, x in enumerate(vectors):
+                nc.scalar.dma_start(
+                    out=vec1_bf[:, v, 0:CH1].rearrange("p (n k) -> p n k", k=PACK), in_=x.rearrange("n (p k) -> p n k", k=PACK)
+                )
 
-        load_vectors((b1, g1, beta1), (b2, g2, beta2), 0)
-        load_t(0)
-        load_vectors((m1, v1), (m2, v2), 3)
-        load_piece(2)
-        w1_codes, w1_planes = load_weight(W1_words, W1_scales, "w1")
-        load_piece(3)
-        load_t(2)
+        def load_vectors2(vectors):
+            for v, x in enumerate(vectors):
+                nc.scalar.dma_start(out=vec2_rows[CH2 * v : CH2 * (v + 1), :], in_=x.rearrange("n (j m) -> (n j) m", m=P))
+
+        load_vectors1((b1, g1, beta1, m1, v1))
+        load_piece(0)
+        w1_raw_codes, w1_raw_planes = load_weight(W1_words, W1_scales, "w1_raw")
+        load_piece(1)
+        load_vectors2((b2, g2, beta2, m2, v2))
+        load_t(1)
         w2_codes, w2_planes = load_weight(W2_words, W2_scales, "w2")
+        load_t(2)
+        load_t(3)
 
+        w1_codes = const.tile([P, BRANCHES * S_PASSES, INTER], U32, align_bytes=64)
+        w1_planes = const.tile([P, INTER], U8, align_bytes=64)
+
+        def move_w1_columns():
+            nc.vector.tensor_copy(
+                out=w1_planes[:].rearrange("p (k m) -> p m k", k=PACK), in_=w1_raw_planes[:].rearrange("p (m k) -> p m k", k=PACK)
+            )
+            for n in range(BRANCHES):
+                passes = slice(S_PASSES * n, S_PASSES * (n + 1))
+                nc.vector.tensor_copy(
+                    out=w1_codes[:, passes, :].bitcast(I32).rearrange("p c (k m) -> p c k m", k=PACK),
+                    in_=w1_raw_codes[:, passes, :].bitcast(I32).rearrange("p c (m k) -> p c k m", k=PACK),
+                )
+
+        vec = const.tile([P, 5, CH], F32)
         factor = const.tile([P, CH], F32)
         offset = const.tile([P, CH], F32)
 
-        def channel_factors():
+        def channel_factors(columns):
+            bias_v, gain_v, beta_v, mean_v, var_v = [vec[:, v, columns] for v in range(5)]
+            nc.vector.tensor_scalar_add(factor[:, columns], var_v, EPS)
+            nc.scalar.sqrt(factor[:, columns], factor[:, columns])
+            nc.vector.reciprocal(factor[:, columns], factor[:, columns])
+            nc.vector.tensor_mul(factor[:, columns], factor[:, columns], gain_v)
+            nc.vector.tensor_sub(offset[:, columns], bias_v, mean_v)
+            nc.vector.tensor_mul(offset[:, columns], offset[:, columns], factor[:, columns])
+            nc.vector.tensor_add(offset[:, columns], offset[:, columns], beta_v)
+
+        def channel_factors1():
+            nc.vector.tensor_copy(out=vec[:, :, 0:CH1], in_=vec1_bf[:, :, 0:CH1])
+            channel_factors(slice(0, CH1))
+
+        def channel_factors2():
             vec_ps = flips.tile([P, P], BF16, tag="flip")
-            nc.tensor.transpose(vec_ps[:], vec_rows[:], ident_bf[:])
-            vec = const.tile([P, P], F32)
-            nc.vector.tensor_copy(out=vec[:], in_=vec_ps[:])
-            bias_v, gain_v, beta_v, mean_v, var_v = [vec[:, CH * v : CH * (v + 1)] for v in range(5)]
-            nc.vector.tensor_scalar_add(factor[:], var_v, EPS)
-            nc.scalar.sqrt(factor[:], factor[:])
-            nc.vector.reciprocal(factor[:], factor[:])
-            nc.vector.tensor_mul(factor[:], factor[:], gain_v)
-            nc.vector.tensor_sub(offset[:], bias_v, mean_v)
-            nc.vector.tensor_mul(offset[:], offset[:], factor[:])
-            nc.vector.tensor_add(offset[:], offset[:], beta_v)
+            nc.tensor.transpose(vec_ps[:], vec2_rows[:], ident_bf[:])
+            nc.vector.tensor_copy(out=vec[:, :, CH1:CH], in_=vec_ps[:, 0 : 5 * CH2].rearrange("p (v c) -> p v c", v=5))
+            channel_factors(slice(CH1, CH))
 
         def as_words(tile3):
             return tile3.rearrange("p x y -> p (x y)").bitcast(F32)
 
-        out_bf = out.bitcast(BF16)
-
-        def parking(half):
-            g, n = divmod(half, BRANCHES)
-            return out_bf[GROUP * g + P * n : GROUP * g + P * (n + 1), :]
-
         s_rows, s_grouped, s_codes, s_planes = {}, {}, {}, {}
-        h_cols, h_lines, h_codes, h_planes = {}, {}, {}, {}
+        h_cols, h_codes, h_planes = {}, {}, {}
         gate_cols, out_sb = {}, {}
 
         def add_branches(piece):
@@ -192,22 +214,11 @@ def tile_af_2_pa_t_e_kernel(
                 )
             h_cols[half] = h_half
 
-        def park_hidden(half):
-            h_half = h_cols[half]
-            nc.scalar.dma_start(
-                out=parking(half).rearrange("r x -> (r x)").rearrange("(j m c) -> m j c", j=INTER // P, m=P), in_=h_half[:]
-            )
-
-        def fetch_hidden(half):
-            lines = work.tile([P, PACK, GROUP], BF16)
-            nc.sync.dma_start(out=lines[:], in_=parking(half).rearrange("p (k c) -> p k c", k=PACK))
-            h_lines[half] = lines
-
         def quantise_hidden(half):
             h_grouped = work.tile([P, GROUP, PACK], BF16, align_bytes=64)
             nc.vector.tensor_copy(
                 out=h_grouped[:].rearrange("p (c i) k -> p c k i", i=4),
-                in_=h_lines[half][:].rearrange("p k (c i) -> p c k i", i=4),
+                in_=h_cols[half][:].rearrange("p k (c i) -> p c k i", i=4),
             )
             h_codes[half] = operands.tile([P, GROUP], U32, align_bytes=64, name="h_codes", tag="h_codes")
             h_planes[half] = operands.tile([P, GROUP], U8, align_bytes=64, name="h_planes", tag="h_planes")
@@ -270,7 +281,7 @@ def tile_af_2_pa_t_e_kernel(
             nc.sync.dma_start(out=out_rows[g][:, :, done], in_=out_sb[g][:, :, done])
 
         S_LEAD = 2
-        GATE_LAG = 4
+        GATE_LAG = 3
 
         def is_half(half):
             return 0 <= half < HALVES
@@ -283,26 +294,22 @@ def tile_af_2_pa_t_e_kernel(
             if 0 <= step + S_LEAD < PIECES:
                 add_branches(step + S_LEAD)
             if step == -S_LEAD:
-                channel_factors()
+                channel_factors1()
+                move_w1_columns()
+                channel_factors2()
             if 0 <= step + S_LEAD - 1 < PIECES:
                 quantise_sum(step + S_LEAD - 1)
             if is_slab(slab):
                 second_layer(slab)
             if is_slab(slab - 1):
                 apply_gates(slab - 1)
-            if is_half(step - 2):
-                quantise_hidden(step - 2)
+            if is_half(step - 1):
+                quantise_hidden(step - 1)
             if is_slab(slab):
                 second_layer(slab + 1)
                 apply_gates(slab)
             if is_half(step):
                 first_layer(step)
-            if is_half(step - 1):
-                fetch_hidden(step - 1)
-            if is_half(step):
-                park_hidden(step)
-            if step == 2:
-                load_t(3)
             if is_slab(slab - 1):
                 store_slab(slab - 1)
             if is_slab(slab):

@@ -55,12 +55,13 @@ def tile_af_2_pa_t_e_kernel(
 
         t_rows = t.rearrange("(g r a) n d -> g r a n d", g=GROUPS, a=ROW_TILES)
         out_rows = out.rearrange("(g r a) d -> g r a d", g=GROUPS, a=ROW_TILES)
-        t_sb = [inputs.tile([P, ROW_TILES, BRANCHES, DIM], BF16, name="t_sb%d" % g) for g in range(GROUPS)]
+        t_sb = [inputs.tile([P, BRANCHES, ROW_TILES, DIM], BF16, name="t_sb%d" % g) for g in range(GROUPS)]
 
         def load_piece(piece):
             g, pair = divmod(piece, 2)
             tiles = slice(2 * pair, 2 * pair + 2)
-            nc.sync.dma_start(out=t_sb[g][:, tiles], in_=t_rows[g][:, tiles])
+            for n in range(BRANCHES):
+                nc.sync.dma_start(out=t_sb[g][:, n, tiles, :], in_=t_rows[g][:, tiles, n, :])
 
         def load_t(g):
             load_piece(2 * g)
@@ -157,21 +158,23 @@ def tile_af_2_pa_t_e_kernel(
         def add_branches(piece):
             g, pair = divmod(piece, 2)
             tiles = slice(2 * pair, 2 * pair + 2)
-            s_pair = work.tile([P, 2, DIM], BF16)
-            nc.vector.tensor_tensor(out=s_pair[:], in0=t_sb[g][:, tiles, 0, :], in1=t_sb[g][:, tiles, 1, :], op=ALU.add)
+            s_pair = work.tile([P, 2, DIM // 2, 2], BF16)
+            terms_in = [
+                t_sb[g][:, n, tiles, :].rearrange("p a d -> p (a d)").rearrange("p (x u e) -> p u x e", u=2, e=2)
+                for n in range(BRANCHES)
+            ]
+            nc.vector.tensor_tensor(out=s_pair[:], in0=terms_in[0], in1=terms_in[1], op=ALU.add)
             s_rows[piece] = s_pair
 
         def transpose_sum(piece):
-            words = as_words(s_rows[piece][:])
+            words = s_rows[piece][:].rearrange("p u x e -> p (u x e)").bitcast(F32)
             grouped = work.tile([P, S_PASSES, PAIR, PACK], BF16, align_bytes=64)
             for c in range(S_PASSES):
                 bank = flips.tile([P, 2, PAIR], F32, tag="flip")
                 for a in range(2):
-                    first = (DIM // 2) * a + (K_PASS // 2) * c
                     for u in range(2):
-                        nc.tensor.transpose(
-                            bank[:, u, P * a : P * (a + 1)], words[:, first + u : first + K_PASS // 2 : 2], ident_f[:]
-                        )
+                        first = (DIM // 2) * u + P * (S_PASSES * a + c)
+                        nc.tensor.transpose(bank[:, u, P * a : P * (a + 1)], words[:, first : first + P], ident_f[:])
                 nc.scalar.copy(
                     out=as_words(grouped[:, c]).rearrange("p (c u) -> p c u", u=2), in_=bank[:].rearrange("p u c -> p c u")
                 )
@@ -269,7 +272,7 @@ def tile_af_2_pa_t_e_kernel(
                     term_sb = terms.tile([P, ROW_TILES, P], F32)
                     term = term_sb[:]
                 nc.vector.scalar_tensor_tensor(
-                    out=term, in0=bank[:], scalar=3.0, in1=t_sb[g][:, :, n, features], op0=ALU.mult, op1=ALU.mult
+                    out=term, in0=bank[:], scalar=3.0, in1=t_sb[g][:, n, :, features], op0=ALU.mult, op1=ALU.mult
                 )
                 if n == 1:
                     nc.gpsimd.tensor_tensor(out=out_sb[g][:, :, features], in0=out_sb[g][:, :, features], in1=term, op=ALU.add)

@@ -272,7 +272,7 @@ def tile_af_2_pa_t_e_kernel(
                     term_sb = terms.tile([P, ROW_TILES, P], F32)
                     term = term_sb[:]
                 nc.vector.scalar_tensor_tensor(
-                    out=term, in0=bank[:], scalar=3.0, in1=t_sb[g][:, n, :, features], op0=ALU.mult, op1=ALU.mult
+                    out=term, in0=t_sb[g][:, n, :, features], scalar=3.0, in1=bank[:], op0=ALU.mult, op1=ALU.mult
                 )
                 if n == 1:
                     nc.gpsimd.tensor_tensor(out=out_sb[g][:, :, features], in0=out_sb[g][:, :, features], in1=term, op=ALU.add)

@@ -50,8 +50,8 @@ def tile_af_2_pa_t_e_kernel(
         operands = ctx.enter_context(tc.tile_pool(name="operands", bufs=4))
         gates = ctx.enter_context(tc.tile_pool(name="gates", bufs=2 * SLAB_TILES * BRANCHES))
         terms = ctx.enter_context(tc.tile_pool(name="terms", bufs=4))
-        sums = ctx.enter_context(tc.psum_pool(name="sums", bufs=4))
-        flips = ctx.enter_context(tc.psum_pool(name="flips", bufs=4))
+        sums = ctx.enter_context(tc.psum_pool(name="banks", bufs=8))
+        flips = sums
 
         t_rows = t.rearrange("(g r a) n d -> g r a n d", g=GROUPS, a=ROW_TILES)
         out_rows = out.rearrange("(g r a) d -> g r a d", g=GROUPS, a=ROW_TILES)
@@ -127,23 +127,27 @@ def tile_af_2_pa_t_e_kernel(
         vec = const.tile([P, 5, CH], F32)
         factor = const.tile([P, CH], F32)
         offset = const.tile([P, CH], F32)
+        minus_half = const.tile([P, CH], F32)
+        nc.gpsimd.memset(minus_half[:], -0.5)
+        warm = const.tile([P, 2], F32)
+        nc.vector.memset(warm[:], 0.0)
+        nc.scalar.activation(out=warm[:, 1:2], in_=warm[:, 0:1], func=ACT.Sigmoid)
 
         def channel_factors(columns):
             bias_v, gain_v, beta_v, mean_v, var_v = [vec[:, v, columns] for v in range(5)]
-            nc.vector.tensor_scalar_add(factor[:, columns], var_v, EPS)
-            nc.scalar.sqrt(factor[:, columns], factor[:, columns])
-            nc.vector.reciprocal(factor[:, columns], factor[:, columns])
-            nc.vector.tensor_mul(factor[:, columns], factor[:, columns], gain_v)
-            nc.vector.tensor_sub(offset[:, columns], bias_v, mean_v)
-            nc.vector.tensor_mul(offset[:, columns], offset[:, columns], factor[:, columns])
-            nc.vector.tensor_add(offset[:, columns], offset[:, columns], beta_v)
+            nc.gpsimd.tensor_scalar_add(factor[:, columns], var_v, EPS)
+            nc.gpsimd.tensor_tensor(out=factor[:, columns], in0=factor[:, columns], in1=minus_half[:, columns], op=ALU.pow)
+            nc.gpsimd.tensor_tensor(out=factor[:, columns], in0=factor[:, columns], in1=gain_v, op=ALU.mult)
+            nc.gpsimd.tensor_tensor(out=offset[:, columns], in0=bias_v, in1=mean_v, op=ALU.subtract)
+            nc.gpsimd.tensor_tensor(out=offset[:, columns], in0=offset[:, columns], in1=factor[:, columns], op=ALU.mult)
+            nc.gpsimd.tensor_tensor(out=offset[:, columns], in0=offset[:, columns], in1=beta_v, op=ALU.add)
 
         def channel_factors1():
-            nc.vector.tensor_copy(out=vec[:, :, 0:CH1], in_=vec1_bf[:, :, 0:CH1])
+            nc.gpsimd.tensor_copy(out=vec[:, :, 0:CH1], in_=vec1_bf[:, :, 0:CH1])
             channel_factors(slice(0, CH1))
 
         def channel_factors2():
-            vec_ps = flips.tile([P, P], BF16, tag="flip")
+            vec_ps = flips.tile([P, P], BF16, tag="bank")
             nc.tensor.transpose(vec_ps[:], vec2_rows[:], ident_bf[:])
             nc.vector.tensor_copy(out=vec[:, :, CH1:CH], in_=vec_ps[:, 0 : 5 * CH2].rearrange("p (v c) -> p v c", v=5))
             channel_factors(slice(CH1, CH))
@@ -170,7 +174,7 @@ def tile_af_2_pa_t_e_kernel(
             words = s_rows[piece][:].rearrange("p u x e -> p (u x e)").bitcast(F32)
             grouped = work.tile([P, S_PASSES, PAIR, PACK], BF16, align_bytes=64)
             for c in range(S_PASSES):
-                bank = flips.tile([P, 2, PAIR], F32, tag="flip")
+                bank = flips.tile([P, 2, PAIR], F32, tag="bank")
                 for a in range(2):
                     for u in range(2):
                         first = (DIM // 2) * u + P * (S_PASSES * a + c)
@@ -198,7 +202,7 @@ def tile_af_2_pa_t_e_kernel(
             h_half = work.tile([P, INTER // P, GROUP], BF16)
             for j in range(INTER // P):
                 channels = slice(P * j, P * (j + 1))
-                acc = sums.tile([P, GROUP], F32, tag="sum")
+                acc = sums.tile([P, GROUP], F32, tag="bank")
                 for c in range(S_PASSES):
                     w = S_PASSES * n + c
                     nc.tensor.matmul_mx(
@@ -239,7 +243,7 @@ def tile_af_2_pa_t_e_kernel(
             g, tiles = slab_tiles(slab)
             for j, n in tiles:
                 features = slice(P * j, P * (j + 1))
-                acc = sums.tile([P, GROUP], F32, tag="sum")
+                acc = sums.tile([P, GROUP], F32, tag="bank")
                 nc.tensor.matmul_mx(
                     out=acc[:],
                     lhsT=w2_codes[:, n, features].bitcast(FP8X4),
@@ -263,7 +267,7 @@ def tile_af_2_pa_t_e_kernel(
                 out_sb[g] = work.tile([P, ROW_TILES, DIM], F32, name="out_sb", tag="out_sb")
             for j, n in tiles:
                 features = slice(P * j, P * (j + 1))
-                bank = flips.tile([P, ROW_TILES, P], F32, tag="flip")
+                bank = flips.tile([P, ROW_TILES, P], F32, tag="bank")
                 for a in range(ROW_TILES):
                     nc.tensor.transpose(bank[:, a, :], gate_cols[(j, n)][:, P * a : P * (a + 1)], ident_f[:])
                 if n == 0:
@@ -275,13 +279,17 @@ def tile_af_2_pa_t_e_kernel(
                     out=term, in0=t_sb[g][:, n, :, features], scalar=3.0, in1=bank[:], op0=ALU.mult, op1=ALU.mult
                 )
                 if n == 1:
-                    nc.gpsimd.tensor_tensor(out=out_sb[g][:, :, features], in0=out_sb[g][:, :, features], in1=term, op=ALU.add)
+                    adder = nc.vector if slab == SLABS - 1 else nc.gpsimd
+                    adder.tensor_tensor(out=out_sb[g][:, :, features], in0=out_sb[g][:, :, features], in1=term, op=ALU.add)
 
         def store_slab(slab):
             g, tiles = slab_tiles(slab)
             first = tiles[0][0]
-            done = slice(P * first, P * (first + SLAB_TILES))
-            nc.sync.dma_start(out=out_rows[g][:, :, done], in_=out_sb[g][:, :, done])
+            parts = SLAB_TILES if slab == SLABS - 1 else 1
+            width = P * SLAB_TILES // parts
+            for part in range(parts):
+                done = slice(P * first + width * part, P * first + width * (part + 1))
+                nc.sync.dma_start(out=out_rows[g][:, :, done], in_=out_sb[g][:, :, done])
 
         S_LEAD = 2
         GATE_LAG = 3
@@ -298,8 +306,8 @@ def tile_af_2_pa_t_e_kernel(
                 add_branches(step + S_LEAD)
             if step == -S_LEAD:
                 channel_factors1()
+            if step == 1 - S_LEAD:
                 move_w1_columns()
-                channel_factors2()
             if 0 <= step + S_LEAD - 1 < PIECES:
                 quantise_sum(step + S_LEAD - 1)
             if is_slab(slab):
@@ -313,6 +321,8 @@ def tile_af_2_pa_t_e_kernel(
                 apply_gates(slab)
             if is_half(step):
                 first_layer(step)
+            if step == 0:
+                channel_factors2()
             if is_slab(slab - 1):
                 store_slab(slab - 1)
             if is_slab(slab):

@@ -32,7 +32,7 @@ CH1 = BRANCHES * INTER // P
 CH2 = BRANCHES * DIM // P
 CH = CH1 + CH2
 D_TILES = DIM // P
-SLAB_TILES = 2
+SLAB_TILES = 1
 GROUP_SLABS = D_TILES // SLAB_TILES
 SLABS = GROUPS * GROUP_SLABS
 
@@ -48,7 +48,7 @@ def tile_af_2_pa_t_e_kernel(
         inputs = ctx.enter_context(tc.tile_pool(name="inputs", bufs=1))
         work = ctx.enter_context(tc.tile_pool(name="work", bufs=2))
         operands = ctx.enter_context(tc.tile_pool(name="operands", bufs=4))
-        gates = ctx.enter_context(tc.tile_pool(name="gates", bufs=2 * SLAB_TILES * BRANCHES))
+        gates = ctx.enter_context(tc.tile_pool(name="gates", bufs=8))
         terms = ctx.enter_context(tc.tile_pool(name="terms", bufs=4))
         sums = ctx.enter_context(tc.psum_pool(name="banks", bufs=8))
         flips = sums
@@ -156,7 +156,7 @@ def tile_af_2_pa_t_e_kernel(
             return tile3.rearrange("p x y -> p (x y)").bitcast(F32)
 
         s_rows, s_grouped, s_codes, s_planes = {}, {}, {}, {}
-        h_cols, h_codes, h_planes = {}, {}, {}
+        h_cols, h_groups, h_codes, h_planes = {}, {}, {}, {}
         gate_cols, out_sb = {}, {}
 
         def add_branches(piece):
@@ -170,10 +170,12 @@ def tile_af_2_pa_t_e_kernel(
             nc.vector.tensor_tensor(out=s_pair[:], in0=terms_in[0], in1=terms_in[1], op=ALU.add)
             s_rows[piece] = s_pair
 
-        def transpose_sum(piece):
+        def transpose_sum(piece, c):
             words = s_rows[piece][:].rearrange("p u x e -> p (u x e)").bitcast(F32)
-            grouped = work.tile([P, S_PASSES, PAIR, PACK], BF16, align_bytes=64)
-            for c in range(S_PASSES):
+            if c == 0:
+                s_grouped[piece] = work.tile([P, S_PASSES, PAIR, PACK], BF16, align_bytes=64, name="s_grouped", tag="s_grouped")
+            grouped = s_grouped[piece]
+            if True:
                 bank = flips.tile([P, 2, PAIR], F32, tag="bank")
                 for a in range(2):
                     for u in range(2):
@@ -182,57 +184,59 @@ def tile_af_2_pa_t_e_kernel(
                 nc.scalar.copy(
                     out=as_words(grouped[:, c]).rearrange("p (c u) -> p c u", u=2), in_=bank[:].rearrange("p u c -> p c u")
                 )
-            s_grouped[piece] = grouped
 
         def quantise_sum(piece):
-            g, pair = divmod(piece, 2)
-            if pair == 0:
-                s_codes[g] = work.tile([P, S_PASSES, GROUP], U32, align_bytes=64, name="s_codes", tag="s_codes")
-                s_planes[g] = work.tile([P, S_PASSES, GROUP], U8, align_bytes=64, name="s_planes", tag="s_planes")
-            columns = slice(PAIR * pair, PAIR * (pair + 1))
-            for c in range(S_PASSES):
-                nc.vector.quantize_mx(
-                    out=s_codes[g][:, c, columns].bitcast(FP8X4),
-                    scales=s_planes[g][:, c, columns],
-                    in_=s_grouped[piece][:, c].rearrange("p c k -> p (c k)"),
-                )
+            s_codes[piece] = operands.tile([P, S_PASSES * PAIR], U32, align_bytes=64, name="s_codes", tag="s_codes")
+            s_planes[piece] = operands.tile([P, S_PASSES * PAIR], U8, align_bytes=64, name="s_planes", tag="s_planes")
+            nc.vector.quantize_mx(
+                out=s_codes[piece][:].bitcast(FP8X4),
+                scales=s_planes[piece][:],
+                in_=s_grouped[piece][:].rearrange("p s c k -> p (s c k)"),
+            )
 
-        def first_layer(half):
+        def first_layer(bank_no):
+            half, j = divmod(bank_no, INTER // P)
             g, n = divmod(half, BRANCHES)
-            h_half = work.tile([P, INTER // P, GROUP], BF16)
-            for j in range(INTER // P):
+            if j == 0:
+                h_cols[half] = work.tile([P, INTER // P, GROUP], BF16, name="h_half", tag="h_half")
+            h_half = h_cols[half]
+            if True:
                 channels = slice(P * j, P * (j + 1))
                 acc = sums.tile([P, GROUP], F32, tag="bank")
-                for c in range(S_PASSES):
-                    w = S_PASSES * n + c
-                    nc.tensor.matmul_mx(
-                        out=acc[:],
-                        lhsT=w1_codes[:, w, channels].bitcast(FP8X4),
-                        lhsT_scale=w1_planes[4 * w : P, channels],
-                        rhs=s_codes[g][:, c, :].bitcast(FP8X4),
-                        rhs_scale=s_planes[g][:, c, :],
-                        start=(c == 0),
-                        stop=(c == S_PASSES - 1),
-                    )
+                for pair in range(2):
+                    for c in range(S_PASSES):
+                        w = S_PASSES * n + c
+                        columns = slice(PAIR * c, PAIR * (c + 1))
+                        nc.tensor.matmul_mx(
+                            out=acc[:, PAIR * pair : PAIR * (pair + 1)],
+                            lhsT=w1_codes[:, w, channels].bitcast(FP8X4),
+                            lhsT_scale=w1_planes[4 * w : P, channels],
+                            rhs=s_codes[2 * g + pair][:, columns].bitcast(FP8X4),
+                            rhs_scale=s_planes[2 * g + pair][:, columns],
+                            start=(c == 0),
+                            stop=(c == S_PASSES - 1),
+                        )
                 ch = (INTER // P) * n + j
                 nc.scalar.activation(
                     out=h_half[:, j, :], in_=acc[:], func=ACT.Relu,
                     bias=offset[:, ch : ch + 1], scale=factor[:, ch : ch + 1],
                 )
-            h_cols[half] = h_half
 
-        def quantise_hidden(half):
+        def regroup_hidden(half):
             h_grouped = work.tile([P, GROUP, PACK], BF16, align_bytes=64)
             nc.vector.tensor_copy(
                 out=h_grouped[:].rearrange("p (c i) k -> p c k i", i=4),
                 in_=h_cols[half][:].rearrange("p k (c i) -> p c k i", i=4),
             )
+            h_groups[half] = h_grouped
+
+        def quantise_hidden(half):
             h_codes[half] = operands.tile([P, GROUP], U32, align_bytes=64, name="h_codes", tag="h_codes")
             h_planes[half] = operands.tile([P, GROUP], U8, align_bytes=64, name="h_planes", tag="h_planes")
             nc.vector.quantize_mx(
                 out=h_codes[half][:].bitcast(FP8X4),
                 scales=h_planes[half][:],
-                in_=h_grouped[:].rearrange("p c k -> p (c k)"),
+                in_=h_groups[half][:].rearrange("p c k -> p (c k)"),
             )
 
         def slab_tiles(slab):
@@ -284,48 +288,34 @@ def tile_af_2_pa_t_e_kernel(
 
         def store_slab(slab):
             g, tiles = slab_tiles(slab)
-            first = tiles[0][0]
-            parts = SLAB_TILES if slab == SLABS - 1 else 1
-            width = P * SLAB_TILES // parts
-            for part in range(parts):
-                done = slice(P * first + width * part, P * first + width * (part + 1))
-                nc.sync.dma_start(out=out_rows[g][:, :, done], in_=out_sb[g][:, :, done])
+            if slab % 2 == 0 and slab < SLABS - 2:
+                return
+            done = slice(P * (tiles[0][0] - 1), P * (tiles[0][0] + 1)) if slab < SLABS - 2 else slice(P * tiles[0][0], P * (tiles[0][0] + 1))
+            nc.sync.dma_start(out=out_rows[g][:, :, done], in_=out_sb[g][:, :, done])
 
-        S_LEAD = 2
-        GATE_LAG = 3
-
-        def is_half(half):
-            return 0 <= half < HALVES
-
-        def is_slab(slab):
-            return 0 <= slab < SLABS
-
-        for step in range(-S_LEAD, HALVES + GATE_LAG + 1):
-            slab = 2 * (step - GATE_LAG)
-            if 0 <= step + S_LEAD < PIECES:
-                add_branches(step + S_LEAD)
-            if step == -S_LEAD:
+        for i in range(-20, SLABS + 1):
+            phase = i % 4
+            piece = (i + 20) // 4
+            half = (i + 12) // 4
+            if phase == 0 and piece < PIECES:
+                add_branches(piece)
+            if i == -20:
                 channel_factors1()
-            if step == 1 - S_LEAD:
                 move_w1_columns()
-            if 0 <= step + S_LEAD - 1 < PIECES:
-                quantise_sum(step + S_LEAD - 1)
-            if is_slab(slab):
-                second_layer(slab)
-            if is_slab(slab - 1):
-                apply_gates(slab - 1)
-            if is_half(step - 1):
-                quantise_hidden(step - 1)
-            if is_slab(slab):
-                second_layer(slab + 1)
-                apply_gates(slab)
-            if is_half(step):
-                first_layer(step)
-            if step == 0:
+            if phase == 1 and 0 <= half - 1 < HALVES:
+                regroup_hidden(half - 1)
+            if phase == 2 and 0 <= half - 1 < HALVES:
+                quantise_hidden(half - 1)
+            if phase == 3 and piece < PIECES:
+                quantise_sum(piece)
+            if 0 <= i < SLABS:
+                second_layer(i)
+            if 0 <= i + 12 < 4 * HALVES:
+                first_layer(i + 12)
+            if i == -5:
                 channel_factors2()
-            if is_slab(slab - 1):
-                store_slab(slab - 1)
-            if is_slab(slab):
-                store_slab(slab)
-            if 0 <= step + S_LEAD < PIECES:
-                transpose_sum(step + S_LEAD)
+            if 0 <= i - 1 < SLABS:
+                apply_gates(i - 1)
+                store_slab(i - 1)
+            if phase in (1, 2) and piece < PIECES:
+                transpose_sum(piece, phase - 1)

@@ -21,20 +21,15 @@ DIM = 1024
 INTER = 512
 EPS = 1e-5
 
-GROUP = 512
-ROW_TILES = GROUP // P
-GROUPS = BATCH // GROUP
-HALVES = GROUPS * BRANCHES
-PIECES = GROUPS * 2
 PAIR = 2 * P
+WIDTHS = (2,) * 8
+GROUPS = len(WIDTHS)
 S_PASSES = DIM // K_PASS
+KS = INTER // P
 CH1 = BRANCHES * INTER // P
 CH2 = BRANCHES * DIM // P
 CH = CH1 + CH2
 D_TILES = DIM // P
-SLAB_TILES = 1
-GROUP_SLABS = D_TILES // SLAB_TILES
-SLABS = GROUPS * GROUP_SLABS
 
 FLOPS = 2 * BATCH * BRANCHES * (DIM * INTER + INTER * DIM)
 
@@ -53,37 +48,46 @@ def tile_af_2_pa_t_e_kernel(
         sums = ctx.enter_context(tc.psum_pool(name="banks", bufs=8))
         flips = sums
 
-        t_rows = t.rearrange("(g r a) n d -> g r a n d", g=GROUPS, a=ROW_TILES)
-        out_rows = out.rearrange("(g r a) d -> g r a d", g=GROUPS, a=ROW_TILES)
-        t_sb = [inputs.tile([P, BRANCHES, ROW_TILES, DIM], BF16, name="t_sb%d" % g) for g in range(GROUPS)]
-
-        def load_piece(piece):
-            g, pair = divmod(piece, 2)
-            tiles = slice(2 * pair, 2 * pair + 2)
-            for n in range(BRANCHES):
-                nc.sync.dma_start(out=t_sb[g][:, n, tiles, :], in_=t_rows[g][:, tiles, n, :])
-
-        def load_t(g):
-            load_piece(2 * g)
-            load_piece(2 * g + 1)
-
-        def load_weight(words, scales, name):
-            passes, columns = words.shape[0], words.shape[2]
-            codes = const.tile([P, passes, columns], U32, align_bytes=64, name=name + "_codes")
-            planes = const.tile([P, columns], U8, align_bytes=64, name=name + "_planes")
-            nc.vector.memset(planes[:].bitcast(I32), 0)
-            nc.sync.dma_start(out=codes[:].bitcast(I32), in_=words.rearrange("c p n k -> p c (n k)").bitcast(I32))
-            for quadrant in range(4):
-                nc.sync.dma_start(
-                    out=planes[32 * quadrant : 32 * quadrant + 4 * passes, :].bitcast(I32),
-                    in_=scales[:, 4 * quadrant : 4 * quadrant + 4, :].bitcast(I32),
-                )
-            return codes, planes
-
         ident_bf = const.tile([P, P], BF16)
         ident_f = const.tile([P, P], F32)
         masks.make_identity(nc, ident_f[:])
         masks.make_identity(nc, ident_bf[:])
+        ctx.enter_context(tc.manual_schedule())
+
+        t_rows, out_rows, first = [], [], 0
+        for a_tiles in WIDTHS:
+            rows = slice(P * first, P * (first + a_tiles))
+            t_rows.append(t[rows].rearrange("(r a) n d -> r a n d", a=a_tiles))
+            out_rows.append(out[rows].rearrange("(r a) d -> r a d", a=a_tiles))
+            first += a_tiles
+        t_sb = [inputs.tile([P, BRANCHES, a_tiles, DIM], BF16, name="t_sb%d" % g) for g, a_tiles in enumerate(WIDTHS)]
+        pieces = [(g, pair) for g, a_tiles in enumerate(WIDTHS) for pair in range(a_tiles // 2)]
+
+        def load_piece(piece):
+            g, pair = pieces[piece]
+            tiles = slice(2 * pair, 2 * pair + 2)
+            for a in (2 * pair, 2 * pair + 1):
+                nc.sync.dma_start(out=t_sb[g][:, :, a, :], in_=t_rows[g][:, a, :, :])
+
+        def weight_tiles(words, name):
+            passes, columns = words.shape[0], words.shape[2]
+            codes = const.tile([P, passes, columns], U32, align_bytes=64, name=name + "_codes")
+            planes = const.tile([P, columns], U8, align_bytes=64, name=name + "_planes")
+            nc.vector.memset(planes[:].bitcast(I32), 0)
+            return codes, planes
+
+        def load_codes(codes, words, passes):
+            nc.sync.dma_start(
+                out=codes[:, passes, :].bitcast(I32), in_=words[passes].rearrange("c p n k -> p c (n k)").bitcast(I32)
+            )
+
+        def load_planes(planes, scales):
+            rows = 4 * scales.shape[0]
+            for quadrant in range(4):
+                nc.sync.dma_start(
+                    out=planes[32 * quadrant : 32 * quadrant + rows, :].bitcast(I32),
+                    in_=scales[:, 4 * quadrant : 4 * quadrant + 4, :].bitcast(I32),
+                )
 
         VEC_PAD = 16
         vec1_bf = const.tile([P, 5, VEC_PAD], BF16)
@@ -98,59 +102,65 @@ def tile_af_2_pa_t_e_kernel(
 
         def load_vectors2(vectors):
             for v, x in enumerate(vectors):
-                nc.scalar.dma_start(out=vec2_rows[CH2 * v : CH2 * (v + 1), :], in_=x.rearrange("n (j m) -> (n j) m", m=P))
+                nc.sync.dma_start(out=vec2_rows[CH2 * v : CH2 * (v + 1), :], in_=x.rearrange("n (j m) -> (n j) m", m=P))
 
         load_vectors1((b1, g1, beta1, m1, v1))
+        w1_raw_codes, w1_raw_planes = weight_tiles(W1_words, "w1_raw")
+        w2_codes, w2_planes = weight_tiles(W2_words, "w2")
         load_piece(0)
-        w1_raw_codes, w1_raw_planes = load_weight(W1_words, W1_scales, "w1_raw")
+        load_codes(w1_raw_codes, W1_words, slice(0, S_PASSES))
+        load_planes(w1_raw_planes, W1_scales)
+        load_codes(w1_raw_codes, W1_words, slice(S_PASSES, 2 * S_PASSES))
         load_piece(1)
         load_vectors2((b2, g2, beta2, m2, v2))
-        load_t(1)
-        w2_codes, w2_planes = load_weight(W2_words, W2_scales, "w2")
-        load_t(2)
-        load_t(3)
+        load_planes(w2_planes, W2_scales)
+        load_codes(w2_codes, W2_words, slice(0, BRANCHES))
+        for piece in range(2, len(pieces)):
+            load_piece(piece)
 
         w1_codes = const.tile([P, BRANCHES * S_PASSES, INTER], U32, align_bytes=64)
         w1_planes = const.tile([P, INTER], U8, align_bytes=64)
 
-        def move_w1_columns():
+        def move_w1_planes():
             nc.vector.tensor_copy(
                 out=w1_planes[:].rearrange("p (k m) -> p m k", k=PACK), in_=w1_raw_planes[:].rearrange("p (m k) -> p m k", k=PACK)
             )
-            for n in range(BRANCHES):
-                passes = slice(S_PASSES * n, S_PASSES * (n + 1))
-                nc.vector.tensor_copy(
-                    out=w1_codes[:, passes, :].bitcast(I32).rearrange("p c (k m) -> p c k m", k=PACK),
-                    in_=w1_raw_codes[:, passes, :].bitcast(I32).rearrange("p c (m k) -> p c k m", k=PACK),
-                )
 
-        vec = const.tile([P, 5, CH], F32)
+        def move_w1_codes(n):
+            passes = slice(S_PASSES * n, S_PASSES * (n + 1))
+            nc.vector.tensor_copy(
+                out=w1_codes[:, passes, :].bitcast(I32).rearrange("p c (k m) -> p c k m", k=PACK),
+                in_=w1_raw_codes[:, passes, :].bitcast(I32).rearrange("p c (m k) -> p c k m", k=PACK),
+            )
+
         factor = const.tile([P, CH], F32)
         offset = const.tile([P, CH], F32)
         minus_half = const.tile([P, CH], F32)
         nc.gpsimd.memset(minus_half[:], -0.5)
+        vec2 = const.tile([P, 5, CH2], F32)
         warm = const.tile([P, 2], F32)
         nc.vector.memset(warm[:], 0.0)
         nc.scalar.activation(out=warm[:, 1:2], in_=warm[:, 0:1], func=ACT.Sigmoid)
 
-        def channel_factors(columns):
-            bias_v, gain_v, beta_v, mean_v, var_v = [vec[:, v, columns] for v in range(5)]
-            nc.gpsimd.tensor_scalar_add(factor[:, columns], var_v, EPS)
-            nc.gpsimd.tensor_tensor(out=factor[:, columns], in0=factor[:, columns], in1=minus_half[:, columns], op=ALU.pow)
-            nc.gpsimd.tensor_tensor(out=factor[:, columns], in0=factor[:, columns], in1=gain_v, op=ALU.mult)
-            nc.gpsimd.tensor_tensor(out=offset[:, columns], in0=bias_v, in1=mean_v, op=ALU.subtract)
-            nc.gpsimd.tensor_tensor(out=offset[:, columns], in0=offset[:, columns], in1=factor[:, columns], op=ALU.mult)
-            nc.gpsimd.tensor_tensor(out=offset[:, columns], in0=offset[:, columns], in1=beta_v, op=ALU.add)
+        def channel_factors(columns, vectors):
+            bias_v, gain_v, beta_v, mean_v, var_v = vectors
+            variance = const.tile([P, CH2], F32, name="variance%d" % columns.start)
+            cols = slice(0, columns.stop - columns.start)
+            nc.vector.tensor_scalar_add(variance[:, cols], var_v, EPS)
+            nc.gpsimd.tensor_tensor(out=factor[:, columns], in0=variance[:, cols], in1=minus_half[:, columns], op=ALU.pow)
+            nc.vector.tensor_tensor(out=offset[:, columns], in0=bias_v, in1=mean_v, op=ALU.subtract)
+            nc.vector.tensor_tensor(out=factor[:, columns], in0=factor[:, columns], in1=gain_v, op=ALU.mult)
+            nc.vector.tensor_tensor(out=offset[:, columns], in0=offset[:, columns], in1=factor[:, columns], op=ALU.mult)
+            nc.vector.tensor_tensor(out=offset[:, columns], in0=offset[:, columns], in1=beta_v, op=ALU.add)
 
         def channel_factors1():
-            nc.gpsimd.tensor_copy(out=vec[:, :, 0:CH1], in_=vec1_bf[:, :, 0:CH1])
-            channel_factors(slice(0, CH1))
+            channel_factors(slice(0, CH1), [vec1_bf[:, v, 0:CH1] for v in range(5)])
 
         def channel_factors2():
             vec_ps = flips.tile([P, P], BF16, tag="bank")
             nc.tensor.transpose(vec_ps[:], vec2_rows[:], ident_bf[:])
-            nc.vector.tensor_copy(out=vec[:, :, CH1:CH], in_=vec_ps[:, 0 : 5 * CH2].rearrange("p (v c) -> p v c", v=5))
-            channel_factors(slice(CH1, CH))
+            nc.vector.tensor_copy(out=vec2[:], in_=vec_ps[:, 0 : 5 * CH2].rearrange("p (v c) -> p v c", v=5))
+            channel_factors(slice(CH1, CH), [vec2[:, v, :] for v in range(5)])
 
         def as_words(tile3):
             return tile3.rearrange("p x y -> p (x y)").bitcast(F32)
@@ -160,14 +170,17 @@ def tile_af_2_pa_t_e_kernel(
         gate_cols, out_sb = {}, {}
 
         def add_branches(piece):
-            g, pair = divmod(piece, 2)
+            g, pair = pieces[piece]
             tiles = slice(2 * pair, 2 * pair + 2)
             s_pair = work.tile([P, 2, DIM // 2, 2], BF16)
-            terms_in = [
-                t_sb[g][:, n, tiles, :].rearrange("p a d -> p (a d)").rearrange("p (x u e) -> p u x e", u=2, e=2)
-                for n in range(BRANCHES)
-            ]
-            nc.vector.tensor_tensor(out=s_pair[:], in0=terms_in[0], in1=terms_in[1], op=ALU.add)
+            for first_tile, last_tile in ((0, 1), (1, 2)) if piece < 1 else ((0, 2),):
+                tiles = slice(2 * pair + first_tile, 2 * pair + last_tile)
+                words = slice(DIM // 4 * first_tile, DIM // 4 * last_tile)
+                terms_in = [
+                    t_sb[g][:, n, tiles, :].rearrange("p a d -> p (a d)").rearrange("p (x u e) -> p u x e", u=2, e=2)
+                    for n in range(BRANCHES)
+                ]
+                nc.vector.tensor_tensor(out=s_pair[:, :, words, :], in0=terms_in[0], in1=terms_in[1], op=ALU.add)
             s_rows[piece] = s_pair
 
         def transpose_sum(piece, c):
@@ -194,128 +207,197 @@ def tile_af_2_pa_t_e_kernel(
                 in_=s_grouped[piece][:].rearrange("p s c k -> p (s c k)"),
             )
 
-        def first_layer(bank_no):
-            half, j = divmod(bank_no, INTER // P)
-            g, n = divmod(half, BRANCHES)
-            if j == 0:
-                h_cols[half] = work.tile([P, INTER // P, GROUP], BF16, name="h_half", tag="h_half")
-            h_half = h_cols[half]
-            if True:
-                channels = slice(P * j, P * (j + 1))
-                acc = sums.tile([P, GROUP], F32, tag="bank")
-                for pair in range(2):
-                    for c in range(S_PASSES):
-                        w = S_PASSES * n + c
-                        columns = slice(PAIR * c, PAIR * (c + 1))
-                        nc.tensor.matmul_mx(
-                            out=acc[:, PAIR * pair : PAIR * (pair + 1)],
-                            lhsT=w1_codes[:, w, channels].bitcast(FP8X4),
-                            lhsT_scale=w1_planes[4 * w : P, channels],
-                            rhs=s_codes[2 * g + pair][:, columns].bitcast(FP8X4),
-                            rhs_scale=s_planes[2 * g + pair][:, columns],
-                            start=(c == 0),
-                            stop=(c == S_PASSES - 1),
-                        )
-                ch = (INTER // P) * n + j
+        def first_layer(unit):
+            g, u = units[unit]
+            wide = WIDTHS[g] == 4
+            cols = P * WIDTHS[g]
+            acc = sums.tile([P, 2, PAIR], F32, name="acc", tag="bank")
+            if wide:
+                n, ks = u // KS, (u % KS,)
+            else:
+                n, ks = u // 2, (2 * (u % 2), 2 * (u % 2) + 1)
+            if u == 0 or (wide and u == KS):
+                h_cols[(g, n)] = work.tile([P, KS, 2 * PAIR], BF16, name="h_half", tag="h_half")
+                if not wide:
+                    h_cols[(g, 1)] = h_cols[(g, 0)]
+            for i in range(2):
+                k = ks[0] if wide else ks[i]
+                channels = slice(P * k, P * (k + 1))
+                piece = pieces.index((g, i if wide else 0))
+                for c in range(S_PASSES):
+                    w = S_PASSES * n + c
+                    columns = slice(PAIR * c, PAIR * (c + 1))
+                    nc.tensor.matmul_mx(
+                        out=acc[:, i, :],
+                        lhsT=w1_codes[:, w, channels].bitcast(FP8X4),
+                        lhsT_scale=w1_planes[4 * w : P, channels],
+                        rhs=s_codes[piece][:, columns].bitcast(FP8X4),
+                        rhs_scale=s_planes[piece][:, columns],
+                        start=(c == 0),
+                        stop=(c == S_PASSES - 1),
+                    )
+            for i, k in enumerate(ks):
+                ch = KS * n + k
+                first_col = 0 if wide else PAIR * n
                 nc.scalar.activation(
-                    out=h_half[:, j, :], in_=acc[:], func=ACT.Relu,
-                    bias=offset[:, ch : ch + 1], scale=factor[:, ch : ch + 1],
+                    out=h_cols[(g, n)][:, k, first_col : first_col + cols],
+                    in_=acc[:].rearrange("p i b -> p (i b)") if wide else acc[:, i, :],
+                    func=ACT.Relu, bias=offset[:, ch : ch + 1], scale=factor[:, ch : ch + 1],
                 )
 
-        def regroup_hidden(half):
-            h_grouped = work.tile([P, GROUP, PACK], BF16, align_bytes=64)
+        def regroup_hidden(quad, part=0, parts=1):
+            if part == 0:
+                h_groups[quad] = work.tile([P, 2 * PAIR, PACK], BF16, align_bytes=64, name="h_grouped", tag="h_grouped")
+            columns = slice(2 * PAIR // parts * part, 2 * PAIR // parts * (part + 1))
             nc.vector.tensor_copy(
-                out=h_grouped[:].rearrange("p (c i) k -> p c k i", i=4),
-                in_=h_cols[half][:].rearrange("p k (c i) -> p c k i", i=4),
+                out=h_groups[quad][:, columns, :].rearrange("p (c i) k -> p c k i", i=4),
+                in_=h_cols[quads[quad]][:, :, columns].rearrange("p k (c i) -> p c k i", i=4),
             )
-            h_groups[half] = h_grouped
 
-        def quantise_hidden(half):
-            h_codes[half] = operands.tile([P, GROUP], U32, align_bytes=64, name="h_codes", tag="h_codes")
-            h_planes[half] = operands.tile([P, GROUP], U8, align_bytes=64, name="h_planes", tag="h_planes")
+        def quantise_hidden(quad):
+            h_codes[quads[quad]] = operands.tile([P, 2 * PAIR], U32, align_bytes=64, name="h_codes", tag="h_codes")
+            h_planes[quads[quad]] = operands.tile([P, 2 * PAIR], U8, align_bytes=64, name="h_planes", tag="h_planes")
             nc.vector.quantize_mx(
-                out=h_codes[half][:].bitcast(FP8X4),
-                scales=h_planes[half][:],
-                in_=h_groups[half][:].rearrange("p c k -> p (c k)"),
+                out=h_codes[quads[quad]][:].bitcast(FP8X4),
+                scales=h_planes[quads[quad]][:],
+                in_=h_groups[quad][:].rearrange("p c k -> p (c k)"),
             )
 
-        def slab_tiles(slab):
-            g, q = divmod(slab, GROUP_SLABS)
-            return g, [(SLAB_TILES * q + i, n) for i in range(SLAB_TILES) for n in range(BRANCHES)]
+        def second_layer(step):
+            g, j0 = steps[step]
+            cols = P * WIDTHS[g]
+            for i in range(2):
+                acc = sums.tile([P, 2 * PAIR], F32, name="acc2", tag="bank")
+                gate = gates.tile([P, 2 * PAIR], F32)
+                for part in range(1 if WIDTHS[g] == 4 else 2):
+                    j, n = (j0, i) if WIDTHS[g] == 4 else (j0 + i, part)
+                    features = slice(P * j, P * (j + 1))
+                    columns = slice(cols * part, cols * (part + 1))
+                    key = (g, n) if WIDTHS[g] == 4 else (g, 0)
+                    nc.tensor.matmul_mx(
+                        out=acc[:, columns],
+                        lhsT=w2_codes[:, n, features].bitcast(FP8X4),
+                        lhsT_scale=w2_planes[4 * n : P, features],
+                        rhs=h_codes[key][:, columns].bitcast(FP8X4),
+                        rhs_scale=h_planes[key][:, columns],
+                        start=True,
+                        stop=True,
+                    )
+                for part in range(1 if WIDTHS[g] == 4 else 2):
+                    j, n = (j0, i) if WIDTHS[g] == 4 else (j0 + i, part)
+                    columns = slice(cols * part, cols * (part + 1))
+                    ch = CH1 + D_TILES * n + j
+                    nc.scalar.activation(
+                        out=gate[:, columns], in_=acc[:, columns], func=ACT.Sigmoid,
+                        bias=offset[:, ch : ch + 1], scale=factor[:, ch : ch + 1],
+                    )
+                gate_cols[(step, i)] = gate
 
-        def second_layer(slab):
-            g, tiles = slab_tiles(slab)
-            for j, n in tiles:
-                features = slice(P * j, P * (j + 1))
-                acc = sums.tile([P, GROUP], F32, tag="bank")
-                nc.tensor.matmul_mx(
-                    out=acc[:],
-                    lhsT=w2_codes[:, n, features].bitcast(FP8X4),
-                    lhsT_scale=w2_planes[4 * n : P, features],
-                    rhs=h_codes[BRANCHES * g + n][:].bitcast(FP8X4),
-                    rhs_scale=h_planes[BRANCHES * g + n][:],
-                    start=True,
-                    stop=True,
-                )
-                ch = CH1 + D_TILES * n + j
-                gate = gates.tile([P, GROUP], F32)
-                nc.scalar.activation(
-                    out=gate[:], in_=acc[:], func=ACT.Sigmoid,
-                    bias=offset[:, ch : ch + 1], scale=factor[:, ch : ch + 1],
-                )
-                gate_cols[(j, n)] = gate
-
-        def apply_gates(slab):
-            g, tiles = slab_tiles(slab)
-            if slab % GROUP_SLABS == 0:
-                out_sb[g] = work.tile([P, ROW_TILES, DIM], F32, name="out_sb", tag="out_sb")
-            for j, n in tiles:
-                features = slice(P * j, P * (j + 1))
-                bank = flips.tile([P, ROW_TILES, P], F32, tag="bank")
-                for a in range(ROW_TILES):
-                    nc.tensor.transpose(bank[:, a, :], gate_cols[(j, n)][:, P * a : P * (a + 1)], ident_f[:])
-                if n == 0:
-                    term = out_sb[g][:, :, features]
+        def apply_gates(step):
+            g, j0 = steps[step]
+            wide = WIDTHS[g] == 4
+            if j0 == 0:
+                out_sb[g] = work.tile([P, 4, DIM], F32, name="out_sb", tag="out_sb")
+            term = terms.tile([P, 2, 4, P], F32, name="term", tag="term")
+            for i in range(2):
+                bank = flips.tile([P, 4, P], F32, tag="bank")
+                for a in range(4):
+                    nc.tensor.transpose(bank[:, a, :], gate_cols[(step, i)][:, P * a : P * (a + 1)], ident_f[:])
+                if wide:
+                    t_in = t_sb[g][:, i, :, P * j0 : P * (j0 + 1)]
                 else:
-                    term_sb = terms.tile([P, ROW_TILES, P], F32)
-                    term = term_sb[:]
+                    t_in = t_sb[g][:].rearrange("p n a d -> p (n a) d")[:, :, P * (j0 + i) : P * (j0 + i + 1)]
                 nc.vector.scalar_tensor_tensor(
-                    out=term, in0=t_sb[g][:, n, :, features], scalar=3.0, in1=bank[:], op0=ALU.mult, op1=ALU.mult
+                    out=term[:, i], in0=t_in, scalar=3.0, in1=bank[:], op0=ALU.mult, op1=ALU.mult
                 )
-                if n == 1:
-                    adder = nc.vector if slab == SLABS - 1 else nc.gpsimd
-                    adder.tensor_tensor(out=out_sb[g][:, :, features], in0=out_sb[g][:, :, features], in1=term, op=ALU.add)
+            adder = nc.vector if step == len(steps) - 1 else nc.gpsimd
+            if wide:
+                adder.tensor_tensor(out=out_sb[g][:, :, P * j0 : P * (j0 + 1)], in0=term[:, 0], in1=term[:, 1], op=ALU.add)
+            else:
+                adder.tensor_tensor(
+                    out=out_sb[g][:, 0:2, P * j0 : P * (j0 + 2)].rearrange("p a (i d) -> p i a d", i=2),
+                    in0=term[:, :, 0:2], in1=term[:, :, 2:4], op=ALU.add,
+                )
 
-        def store_slab(slab):
-            g, tiles = slab_tiles(slab)
-            if slab % 2 == 0 and slab < SLABS - 2:
-                return
-            done = slice(P * (tiles[0][0] - 1), P * (tiles[0][0] + 1)) if slab < SLABS - 2 else slice(P * tiles[0][0], P * (tiles[0][0] + 1))
-            nc.sync.dma_start(out=out_rows[g][:, :, done], in_=out_sb[g][:, :, done])
+        def store(step):
+            g, j0 = steps[step]
+            if step == len(steps) - 1:
+                done = slice(P * j0, DIM)
+            elif step == len(steps) - 2:
+                done = slice(P * (j0 - (j0 % 2)), P * (j0 + 1)) if WIDTHS[g] == 4 else slice(P * j0, P * (j0 + 2))
+            elif WIDTHS[g] == 4:
+                if j0 % 2 == 0:
+                    return
+                done = slice(P * (j0 - 1), P * (j0 + 1))
+            else:
+                done = slice(P * j0, P * (j0 + 2))
+            nc.sync.dma_start(out=out_rows[g][:, :, done], in_=out_sb[g][:, 0 : WIDTHS[g], done])
 
-        for i in range(-20, SLABS + 1):
-            phase = i % 4
-            piece = (i + 20) // 4
-            half = (i + 12) // 4
-            if phase == 0 and piece < PIECES:
-                add_branches(piece)
-            if i == -20:
-                channel_factors1()
-                move_w1_columns()
-            if phase == 1 and 0 <= half - 1 < HALVES:
-                regroup_hidden(half - 1)
-            if phase == 2 and 0 <= half - 1 < HALVES:
-                quantise_hidden(half - 1)
-            if phase == 3 and piece < PIECES:
-                quantise_sum(piece)
-            if 0 <= i < SLABS:
-                second_layer(i)
-            if 0 <= i + 12 < 4 * HALVES:
-                first_layer(i + 12)
-            if i == -5:
-                channel_factors2()
-            if 0 <= i - 1 < SLABS:
-                apply_gates(i - 1)
-                store_slab(i - 1)
-            if phase in (1, 2) and piece < PIECES:
-                transpose_sum(piece, phase - 1)
+        units = [(g, u) for g in range(GROUPS) for u in range(2 * WIDTHS[g])]
+        steps = [(g, j) for g in range(GROUPS) for j in range(0, D_TILES, 4 // WIDTHS[g])]
+        quads = []
+        for g in range(GROUPS):
+            quads += [(g, 0), (g, 1)] if WIDTHS[g] == 4 else [(g, 0)]
+        QUADS = len(quads)
+
+        add_branches(0)
+        transpose_sum(0, 0)
+        transpose_sum(0, 1)
+        move_w1_planes()
+        move_w1_codes(0)
+        quantise_sum(0)
+        channel_factors1()
+        first_layer(0)
+        first_layer(1)
+        move_w1_codes(1)
+        first_layer(2)
+        first_layer(3)
+        add_branches(1)
+        regroup_hidden(0, 0, 2)
+        transpose_sum(1, 0)
+        transpose_sum(1, 1)
+        regroup_hidden(0, 1, 2)
+        quantise_hidden(0)
+        channel_factors2()
+        quantise_sum(1)
+
+        unit_steps = [0, 0, 1, 1, 4, 4, 5, 5] + [4 * g - 7 + u for g in range(3, 8) for u in range(4)]
+        add_step = {g: {2: 0, 3: 1, 4: 4}.get(g, 4 * g - 13) for g in range(2, 8)}
+        qs_step = {g: max(4 * g - 8, add_step[g] + 3) for g in range(2, 8)}
+        rg_step = {g: unit_steps[4 * (g - 1) + 3] + 1 for g in range(1, 8)}
+        for step in range(len(steps) + 1):
+            def vector_work():
+                for g in range(1, 8):
+                    if rg_step[g] == step - 1:
+                        quantise_hidden(g)
+                for g in range(1, 8):
+                    if rg_step[g] == step:
+                        regroup_hidden(g)
+                for g in range(2, 8):
+                    if qs_step[g] == step:
+                        quantise_sum(g)
+                for g in range(2, 8):
+                    if add_step[g] == step:
+                        add_branches(g)
+
+            def layer1():
+                for i in range(28):
+                    if unit_steps[i] == step:
+                        first_layer(4 + i)
+
+            def flips_s():
+                for g in range(2, 8):
+                    if step - add_step[g] in (1, 2):
+                        transpose_sum(g, (1, 2).index(step - add_step[g]))
+            def layer2():
+                if step < len(steps):
+                    second_layer(step)
+            def gates_():
+                if step > 0:
+                    apply_gates(step - 1)
+                    store(step - 1)
+            vector_work()
+            layer2()
+            layer1()
+            gates_()
+            flips_s()

@@ -22,7 +22,7 @@ INTER = 512
 EPS = 1e-5
 
 PAIR = 2 * P
-WIDTHS = (2,) * 8
+WIDTHS = (2, 2, 2, 2, 2, 2, 2, 2)
 GROUPS = len(WIDTHS)
 S_PASSES = DIM // K_PASS
 KS = INTER // P
@@ -156,9 +156,12 @@ def tile_af_2_pa_t_e_kernel(
         def channel_factors1():
             channel_factors(slice(0, CH1), [vec1_bf[:, v, 0:CH1] for v in range(5)])
 
-        def channel_factors2():
+        def transpose_vectors2():
             vec_ps = flips.tile([P, P], BF16, tag="bank")
             nc.tensor.transpose(vec_ps[:], vec2_rows[:], ident_bf[:])
+            return vec_ps
+
+        def channel_factors2(vec_ps):
             nc.vector.tensor_copy(out=vec2[:], in_=vec_ps[:, 0 : 5 * CH2].rearrange("p (v c) -> p v c", v=5))
             channel_factors(slice(CH1, CH), [vec2[:, v, :] for v in range(5)])
 
@@ -167,7 +170,10 @@ def tile_af_2_pa_t_e_kernel(
 
         s_rows, s_grouped, s_codes, s_planes = {}, {}, {}, {}
         h_cols, h_groups, h_codes, h_planes = {}, {}, {}, {}
-        gate_cols, out_sb = {}, {}
+        gate_cols, out_sb, term_sb = {}, {}, {}
+
+        def on_vector(step):
+            return step == len(steps) - 1 or step >= 28 and step % 2 == 1
 
         def add_branches(piece):
             g, pair = pieces[piece]
@@ -254,13 +260,15 @@ def tile_af_2_pa_t_e_kernel(
                 in_=h_cols[quads[quad]][:, :, columns].rearrange("p k (c i) -> p c k i", i=4),
             )
 
-        def quantise_hidden(quad):
-            h_codes[quads[quad]] = operands.tile([P, 2 * PAIR], U32, align_bytes=64, name="h_codes", tag="h_codes")
-            h_planes[quads[quad]] = operands.tile([P, 2 * PAIR], U8, align_bytes=64, name="h_planes", tag="h_planes")
+        def quantise_hidden(quad, part=0, parts=1):
+            if part == 0:
+                h_codes[quads[quad]] = operands.tile([P, 2 * PAIR], U32, align_bytes=64, name="h_codes", tag="h_codes")
+                h_planes[quads[quad]] = operands.tile([P, 2 * PAIR], U8, align_bytes=64, name="h_planes", tag="h_planes")
+            columns = slice(2 * PAIR // parts * part, 2 * PAIR // parts * (part + 1))
             nc.vector.quantize_mx(
-                out=h_codes[quads[quad]][:].bitcast(FP8X4),
-                scales=h_planes[quads[quad]][:],
-                in_=h_groups[quad][:].rearrange("p c k -> p (c k)"),
+                out=h_codes[quads[quad]][:, columns].bitcast(FP8X4),
+                scales=h_planes[quads[quad]][:, columns],
+                in_=h_groups[quad][:, columns, :].rearrange("p c k -> p (c k)"),
             )
 
         def second_layer(step):
@@ -310,7 +318,13 @@ def tile_af_2_pa_t_e_kernel(
                 nc.vector.scalar_tensor_tensor(
                     out=term[:, i], in0=t_in, scalar=3.0, in1=bank[:], op0=ALU.mult, op1=ALU.mult
                 )
-            adder = nc.vector if step == len(steps) - 1 else nc.gpsimd
+            term_sb[step] = term
+
+        def add_terms(step):
+            g, j0 = steps[step]
+            wide = WIDTHS[g] == 4
+            term = term_sb[step]
+            adder = nc.vector if on_vector(step) else nc.gpsimd
             if wide:
                 adder.tensor_tensor(out=out_sb[g][:, :, P * j0 : P * (j0 + 1)], in0=term[:, 0], in1=term[:, 1], op=ALU.add)
             else:
@@ -340,62 +354,77 @@ def tile_af_2_pa_t_e_kernel(
             quads += [(g, 0), (g, 1)] if WIDTHS[g] == 4 else [(g, 0)]
         QUADS = len(quads)
 
+        dummy = const.tile([P, 512], BF16)
+        nc.vector.memset(dummy[:], 0.0)
+        warm_ps = sums.tile([P, 512], F32, name="warm_ps", tag="bank")
         add_branches(0)
+        for dummy_pass in range(4):
+            nc.tensor.matmul(warm_ps[:], lhsT=ident_bf[:], rhs=dummy[:], start=True, stop=True)
         transpose_sum(0, 0)
         transpose_sum(0, 1)
+        for dummy_pass in range(4):
+            nc.tensor.matmul(warm_ps[:], lhsT=ident_bf[:], rhs=dummy[:], start=True, stop=True)
+        vectors2 = transpose_vectors2()
         move_w1_planes()
         move_w1_codes(0)
-        quantise_sum(0)
         channel_factors1()
+        quantise_sum(0)
         first_layer(0)
         first_layer(1)
         move_w1_codes(1)
         first_layer(2)
         first_layer(3)
+        channel_factors2(vectors2)
         add_branches(1)
         regroup_hidden(0, 0, 2)
         transpose_sum(1, 0)
         transpose_sum(1, 1)
         regroup_hidden(0, 1, 2)
-        quantise_hidden(0)
-        channel_factors2()
+        quantise_hidden(0, 0, 2)
+        quantise_hidden(0, 1, 2)
         quantise_sum(1)
 
-        unit_steps = [0, 0, 1, 1, 4, 4, 5, 5] + [4 * g - 7 + u for g in range(3, 8) for u in range(4)]
-        add_step = {g: {2: 0, 3: 1, 4: 4}.get(g, 4 * g - 13) for g in range(2, 8)}
-        qs_step = {g: max(4 * g - 8, add_step[g] + 3) for g in range(2, 8)}
-        rg_step = {g: unit_steps[4 * (g - 1) + 3] + 1 for g in range(1, 8)}
+        unit_steps = [0, 0, 1, 1, 4, 4, 5, 5] + [4 * q - 7 + u for q in range(3, 8) for u in range(4)]
+        add_step = {2: 0, 3: 1, 4: 4, 5: 7, 6: 11, 7: 15}
+        qs_step = {2: 3, 3: 4, 4: 8, 5: 12, 6: 16, 7: 20}
+        rg_step = {q: unit_steps[4 * (q - 1) + 3] + 1 for q in range(1, len(quads))}
         for step in range(len(steps) + 1):
             def vector_work():
-                for g in range(1, 8):
-                    if rg_step[g] == step - 1:
-                        quantise_hidden(g)
-                for g in range(1, 8):
-                    if rg_step[g] == step:
-                        regroup_hidden(g)
-                for g in range(2, 8):
-                    if qs_step[g] == step:
-                        quantise_sum(g)
-                for g in range(2, 8):
-                    if add_step[g] == step:
-                        add_branches(g)
+                if step > 1 and on_vector(step - 2):
+                    add_terms(step - 2)
+                    store(step - 2)
+                for q in rg_step:
+                    if rg_step[q] + 1 == step:
+                        quantise_hidden(q)
+                for q in rg_step:
+                    if rg_step[q] == step:
+                        regroup_hidden(q)
+                for piece in add_step:
+                    if qs_step[piece] == step:
+                        quantise_sum(piece)
+                for piece in add_step:
+                    if add_step[piece] == step:
+                        add_branches(piece)
 
             def layer1():
-                for i in range(28):
+                for i in range(len(unit_steps)):
                     if unit_steps[i] == step:
                         first_layer(4 + i)
 
             def flips_s():
-                for g in range(2, 8):
-                    if step - add_step[g] in (1, 2):
-                        transpose_sum(g, (1, 2).index(step - add_step[g]))
+                for piece in add_step:
+                    for c in range(2):
+                        if step == add_step[piece] + (1, 2)[c]:
+                            transpose_sum(piece, c)
             def layer2():
                 if step < len(steps):
                     second_layer(step)
             def gates_():
                 if step > 0:
                     apply_gates(step - 1)
-                    store(step - 1)
+                    if not on_vector(step - 1) or step == len(steps):
+                        add_terms(step - 1)
+                        store(step - 1)
             vector_work()
             layer2()
             layer1()

@@ -142,28 +142,36 @@ def tile_af_2_pa_t_e_kernel(
         nc.vector.memset(warm[:], 0.0)
         nc.scalar.activation(out=warm[:, 1:2], in_=warm[:, 0:1], func=ACT.Sigmoid)
 
-        def channel_factors(columns, vectors):
+        def factor_steps(columns, vectors):
             bias_v, gain_v, beta_v, mean_v, var_v = vectors
             variance = const.tile([P, CH2], F32, name="variance%d" % columns.start)
             cols = slice(0, columns.stop - columns.start)
-            nc.vector.tensor_scalar_add(variance[:, cols], var_v, EPS)
-            nc.gpsimd.tensor_tensor(out=factor[:, columns], in0=variance[:, cols], in1=minus_half[:, columns], op=ALU.pow)
-            nc.vector.tensor_tensor(out=offset[:, columns], in0=bias_v, in1=mean_v, op=ALU.subtract)
-            nc.vector.tensor_tensor(out=factor[:, columns], in0=factor[:, columns], in1=gain_v, op=ALU.mult)
-            nc.vector.tensor_tensor(out=offset[:, columns], in0=offset[:, columns], in1=factor[:, columns], op=ALU.mult)
-            nc.vector.tensor_tensor(out=offset[:, columns], in0=offset[:, columns], in1=beta_v, op=ALU.add)
 
-        def channel_factors1():
-            channel_factors(slice(0, CH1), [vec1_bf[:, v, 0:CH1] for v in range(5)])
+            def first():
+                nc.vector.tensor_scalar_add(variance[:, cols], var_v, EPS)
+                nc.gpsimd.tensor_tensor(out=factor[:, columns], in0=variance[:, cols], in1=minus_half[:, columns], op=ALU.pow)
+
+            def second():
+                nc.vector.tensor_tensor(out=offset[:, columns], in0=bias_v, in1=mean_v, op=ALU.subtract)
+
+            def third():
+                nc.vector.tensor_tensor(out=factor[:, columns], in0=factor[:, columns], in1=gain_v, op=ALU.mult)
+
+            def fourth():
+                nc.vector.tensor_tensor(out=offset[:, columns], in0=offset[:, columns], in1=factor[:, columns], op=ALU.mult)
+
+            def fifth():
+                nc.vector.tensor_tensor(out=offset[:, columns], in0=offset[:, columns], in1=beta_v, op=ALU.add)
+
+            return first, second, third, fourth, fifth
 
         def transpose_vectors2():
             vec_ps = flips.tile([P, P], BF16, tag="bank")
             nc.tensor.transpose(vec_ps[:], vec2_rows[:], ident_bf[:])
             return vec_ps
 
-        def channel_factors2(vec_ps):
+        def copy_vectors2(vec_ps):
             nc.vector.tensor_copy(out=vec2[:], in_=vec_ps[:, 0 : 5 * CH2].rearrange("p (v c) -> p v c", v=5))
-            channel_factors(slice(CH1, CH), [vec2[:, v, :] for v in range(5)])
 
         def as_words(tile3):
             return tile3.rearrange("p x y -> p (x y)").bitcast(F32)
@@ -173,7 +181,7 @@ def tile_af_2_pa_t_e_kernel(
         gate_cols, out_sb, term_sb = {}, {}, {}
 
         def on_vector(step):
-            return step == len(steps) - 1 or step >= 28 and step % 2 == 1
+            return step == len(steps) - 1 or False
 
         def add_branches(piece):
             g, pair = pieces[piece]
@@ -328,15 +336,17 @@ def tile_af_2_pa_t_e_kernel(
             if wide:
                 adder.tensor_tensor(out=out_sb[g][:, :, P * j0 : P * (j0 + 1)], in0=term[:, 0], in1=term[:, 1], op=ALU.add)
             else:
-                adder.tensor_tensor(
-                    out=out_sb[g][:, 0:2, P * j0 : P * (j0 + 2)].rearrange("p a (i d) -> p i a d", i=2),
-                    in0=term[:, :, 0:2], in1=term[:, :, 2:4], op=ALU.add,
-                )
+                out_tiles = out_sb[g][:, 0:2, P * j0 : P * (j0 + 2)].rearrange("p a (i d) -> p i a d", i=2)
+                for tiles in (slice(0, 1), slice(1, 2)) if step == len(steps) - 1 else (slice(0, 2),):
+                    adder.tensor_tensor(out=out_tiles[:, tiles], in0=term[:, tiles, 0:2], in1=term[:, tiles, 2:4], op=ALU.add)
 
         def store(step):
             g, j0 = steps[step]
             if step == len(steps) - 1:
-                done = slice(P * j0, DIM)
+                for j in (j0, j0 + 1):
+                    done = slice(P * j, P * (j + 1))
+                    nc.sync.dma_start(out=out_rows[g][:, :, done], in_=out_sb[g][:, 0 : WIDTHS[g], done])
+                return
             elif step == len(steps) - 2:
                 done = slice(P * (j0 - (j0 % 2)), P * (j0 + 1)) if WIDTHS[g] == 4 else slice(P * j0, P * (j0 + 2))
             elif WIDTHS[g] == 4:
@@ -357,29 +367,40 @@ def tile_af_2_pa_t_e_kernel(
         dummy = const.tile([P, 512], BF16)
         nc.vector.memset(dummy[:], 0.0)
         warm_ps = sums.tile([P, 512], F32, name="warm_ps", tag="bank")
+        factors1 = factor_steps(slice(0, CH1), [vec1_bf[:, v, 0:CH1] for v in range(5)])
+        factors2 = factor_steps(slice(CH1, CH), [vec2[:, v, :] for v in range(5)])
         add_branches(0)
         for dummy_pass in range(4):
             nc.tensor.matmul(warm_ps[:], lhsT=ident_bf[:], rhs=dummy[:], start=True, stop=True)
         transpose_sum(0, 0)
         transpose_sum(0, 1)
-        for dummy_pass in range(4):
+        for dummy_pass in range(2):
             nc.tensor.matmul(warm_ps[:], lhsT=ident_bf[:], rhs=dummy[:], start=True, stop=True)
         vectors2 = transpose_vectors2()
         move_w1_planes()
+        factors1[0]()
         move_w1_codes(0)
-        channel_factors1()
+        factors1[1]()
+        factors1[2]()
         quantise_sum(0)
+        factors1[3]()
+        copy_vectors2(vectors2)
+        factors1[4]()
         first_layer(0)
         first_layer(1)
         move_w1_codes(1)
         first_layer(2)
         first_layer(3)
-        channel_factors2(vectors2)
+        factors2[0]()
+        factors2[1]()
         add_branches(1)
+        factors2[2]()
         regroup_hidden(0, 0, 2)
+        factors2[3]()
         transpose_sum(1, 0)
         transpose_sum(1, 1)
         regroup_hidden(0, 1, 2)
+        factors2[4]()
         quantise_hidden(0, 0, 2)
         quantise_hidden(0, 1, 2)
         quantise_sum(1)

@@ -197,20 +197,17 @@ def tile_af_2_pa_t_e_kernel(
                 nc.vector.tensor_tensor(out=s_pair[:, :, words, :], in0=terms_in[0], in1=terms_in[1], op=ALU.add)
             s_rows[piece] = s_pair
 
-        def transpose_sum(piece, c):
+        def transpose_sum(piece, a):
             words = s_rows[piece][:].rearrange("p u x e -> p (u x e)").bitcast(F32)
-            if c == 0:
+            if a == 0:
                 s_grouped[piece] = work.tile([P, S_PASSES, PAIR, PACK], BF16, align_bytes=64, name="s_grouped", tag="s_grouped")
-            grouped = s_grouped[piece]
-            if True:
-                bank = flips.tile([P, 2, PAIR], F32, tag="bank")
-                for a in range(2):
-                    for u in range(2):
-                        first = (DIM // 2) * u + P * (S_PASSES * a + c)
-                        nc.tensor.transpose(bank[:, u, P * a : P * (a + 1)], words[:, first : first + P], ident_f[:])
-                nc.scalar.copy(
-                    out=as_words(grouped[:, c]).rearrange("p (c u) -> p c u", u=2), in_=bank[:].rearrange("p u c -> p c u")
-                )
+            bank = flips.tile([P, S_PASSES, 2, P], F32, tag="bank")
+            for c in range(S_PASSES):
+                for u in range(2):
+                    first = (DIM // 2) * u + P * (S_PASSES * a + c)
+                    nc.tensor.transpose(bank[:, c, u, :], words[:, first : first + P], ident_f[:])
+            grouped = s_grouped[piece][:].rearrange("p c r k -> p c (r k)").bitcast(F32).rearrange("p c (r u) -> p c r u", u=2)
+            nc.scalar.copy(out=grouped[:, :, P * a : P * (a + 1), :], in_=bank[:].rearrange("p c u r -> p c r u"))
 
         def quantise_sum(piece):
             s_codes[piece] = operands.tile([P, S_PASSES * PAIR], U32, align_bytes=64, name="s_codes", tag="s_codes")
@@ -367,47 +364,52 @@ def tile_af_2_pa_t_e_kernel(
         dummy = const.tile([P, 512], BF16)
         nc.vector.memset(dummy[:], 0.0)
         warm_ps = sums.tile([P, 512], F32, name="warm_ps", tag="bank")
+
+        def warm_up(count):
+            for dummy_pass in range(count):
+                nc.tensor.matmul(warm_ps[:], lhsT=ident_bf[:], rhs=dummy[:], start=True, stop=True)
+
         factors1 = factor_steps(slice(0, CH1), [vec1_bf[:, v, 0:CH1] for v in range(5)])
         factors2 = factor_steps(slice(CH1, CH), [vec2[:, v, :] for v in range(5)])
         add_branches(0)
-        for dummy_pass in range(4):
-            nc.tensor.matmul(warm_ps[:], lhsT=ident_bf[:], rhs=dummy[:], start=True, stop=True)
+        warm_up(4)
         transpose_sum(0, 0)
         transpose_sum(0, 1)
-        for dummy_pass in range(2):
-            nc.tensor.matmul(warm_ps[:], lhsT=ident_bf[:], rhs=dummy[:], start=True, stop=True)
+        warm_up(2)
         vectors2 = transpose_vectors2()
-        move_w1_planes()
         factors1[0]()
-        move_w1_codes(0)
+        move_w1_planes()
         factors1[1]()
-        factors1[2]()
+        move_w1_codes(0)
         quantise_sum(0)
-        factors1[3]()
+        factors1[2]()
         copy_vectors2(vectors2)
+        factors1[3]()
+        factors2[0]()
         factors1[4]()
         first_layer(0)
         first_layer(1)
         move_w1_codes(1)
         first_layer(2)
         first_layer(3)
-        factors2[0]()
         factors2[1]()
         add_branches(1)
-        factors2[2]()
         regroup_hidden(0, 0, 2)
-        factors2[3]()
         transpose_sum(1, 0)
         transpose_sum(1, 1)
+        warm_ps = sums.tile([P, 512], F32, name="warm_ps", tag="bank")
+        warm_up(2)
         regroup_hidden(0, 1, 2)
-        factors2[4]()
+        factors2[2]()
         quantise_hidden(0, 0, 2)
+        factors2[3]()
         quantise_hidden(0, 1, 2)
+        factors2[4]()
         quantise_sum(1)
 
-        unit_steps = [0, 0, 1, 1, 4, 4, 5, 5] + [4 * q - 7 + u for q in range(3, 8) for u in range(4)]
+        unit_steps = [0, 0, 1, 1, 3, 3, 4, 4, 5, 6, 7, 8] + [4 * q - 7 + u for q in range(4, 8) for u in range(4)]
         add_step = {2: 0, 3: 1, 4: 4, 5: 7, 6: 11, 7: 15}
-        qs_step = {2: 3, 3: 4, 4: 8, 5: 12, 6: 16, 7: 20}
+        qs_step = {2: 2, 3: 3, 4: 8, 5: 12, 6: 16, 7: 20}
         rg_step = {q: unit_steps[4 * (q - 1) + 3] + 1 for q in range(1, len(quads))}
         for step in range(len(steps) + 1):
             def vector_work():
@@ -435,7 +437,7 @@ def tile_af_2_pa_t_e_kernel(
             def flips_s():
                 for piece in add_step:
                     for c in range(2):
-                        if step == add_step[piece] + (1, 2)[c]:
+                        if step == add_step[piece] + (1, 1)[c]:
                             transpose_sum(piece, c)
             def layer2():
                 if step < len(steps):

from contextlib import ExitStack

import concourse.masks as masks
import concourse.mybir as mybir

F32 = mybir.dt.float32
BF16 = mybir.dt.bfloat16
I32 = mybir.dt.int32
U32 = mybir.dt.uint32
U8 = mybir.dt.uint8
FP8X4 = mybir.dt.float8_e4m3fn_x4
ACT = mybir.ActivationFunctionType
ALU = mybir.AluOpType

P = 128
PACK = 4
K_PASS = P * PACK
BATCH = 2048
BRANCHES = 2
DIM = 1024
INTER = 512
EPS = 1e-5

PAIR = 2 * P
WIDTHS = (2, 2, 2, 2, 2, 2, 2, 2)
GROUPS = len(WIDTHS)
S_PASSES = DIM // K_PASS
KS = INTER // P
CH1 = BRANCHES * INTER // P
CH2 = BRANCHES * DIM // P
CH = CH1 + CH2
D_TILES = DIM // P

FLOPS = 2 * BATCH * BRANCHES * (DIM * INTER + INTER * DIM)


def tile_af_2_pa_t_e_kernel(
    tc, t, W1_words, W1_scales, b1, g1, beta1, m1, v1, W2_words, W2_scales, b2, g2, beta2, m2, v2, out
):
    nc = tc.nc
    with ExitStack() as ctx:
        const = ctx.enter_context(tc.tile_pool(name="const", bufs=1))
        inputs = ctx.enter_context(tc.tile_pool(name="inputs", bufs=1))
        work = ctx.enter_context(tc.tile_pool(name="work", bufs=2))
        operands = ctx.enter_context(tc.tile_pool(name="operands", bufs=4))
        gates = ctx.enter_context(tc.tile_pool(name="gates", bufs=8))
        terms = ctx.enter_context(tc.tile_pool(name="terms", bufs=4))
        sums = ctx.enter_context(tc.psum_pool(name="banks", bufs=8))
        flips = sums

        ident_bf = const.tile([P, P], BF16)
        ident_f = const.tile([P, P], F32)
        masks.make_identity(nc, ident_f[:])
        masks.make_identity(nc, ident_bf[:])
        ctx.enter_context(tc.manual_schedule())

        t_rows, out_rows, first = [], [], 0
        for a_tiles in WIDTHS:
            rows = slice(P * first, P * (first + a_tiles))
            t_rows.append(t[rows].rearrange("(r a) n d -> r a n d", a=a_tiles))
            out_rows.append(out[rows].rearrange("(r a) d -> r a d", a=a_tiles))
            first += a_tiles
        t_sb = [inputs.tile([P, BRANCHES, a_tiles, DIM], BF16, name="t_sb%d" % g) for g, a_tiles in enumerate(WIDTHS)]
        pieces = [(g, pair) for g, a_tiles in enumerate(WIDTHS) for pair in range(a_tiles // 2)]

        def load_piece(piece):
            g, pair = pieces[piece]
            tiles = slice(2 * pair, 2 * pair + 2)
            for a in (2 * pair, 2 * pair + 1):
                nc.sync.dma_start(out=t_sb[g][:, :, a, :], in_=t_rows[g][:, a, :, :])

        def weight_tiles(words, name):
            passes, columns = words.shape[0], words.shape[2]
            codes = const.tile([P, passes, columns], U32, align_bytes=64, name=name + "_codes")
            planes = const.tile([P, columns], U8, align_bytes=64, name=name + "_planes")
            nc.vector.memset(planes[:].bitcast(I32), 0)
            return codes, planes

        def load_codes(codes, words, passes):
            nc.sync.dma_start(
                out=codes[:, passes, :].bitcast(I32), in_=words[passes].rearrange("c p n k -> p c (n k)").bitcast(I32)
            )

        def load_planes(planes, scales):
            rows = 4 * scales.shape[0]
            for quadrant in range(4):
                nc.sync.dma_start(
                    out=planes[32 * quadrant : 32 * quadrant + rows, :].bitcast(I32),
                    in_=scales[:, 4 * quadrant : 4 * quadrant + 4, :].bitcast(I32),
                )

        VEC_PAD = 16
        vec1_bf = const.tile([P, 5, VEC_PAD], BF16)
        vec2_rows = const.tile([P, P], BF16)
        nc.vector.memset(vec2_rows[:], 0.0)

        def load_vectors1(vectors):
            for v, x in enumerate(vectors):
                nc.scalar.dma_start(
                    out=vec1_bf[:, v, 0:CH1].rearrange("p (n k) -> p n k", k=PACK), in_=x.rearrange("n (p k) -> p n k", k=PACK)
                )

        def load_vectors2(vectors):
            for v, x in enumerate(vectors):
                nc.sync.dma_start(out=vec2_rows[CH2 * v : CH2 * (v + 1), :], in_=x.rearrange("n (j m) -> (n j) m", m=P))

        load_vectors1((b1, g1, beta1, m1, v1))
        w1_raw_codes, w1_raw_planes = weight_tiles(W1_words, "w1_raw")
        w2_codes, w2_planes = weight_tiles(W2_words, "w2")
        load_piece(0)
        load_codes(w1_raw_codes, W1_words, slice(0, S_PASSES))
        load_planes(w1_raw_planes, W1_scales)
        load_codes(w1_raw_codes, W1_words, slice(S_PASSES, 2 * S_PASSES))
        load_piece(1)
        load_vectors2((b2, g2, beta2, m2, v2))
        load_planes(w2_planes, W2_scales)
        load_codes(w2_codes, W2_words, slice(0, BRANCHES))
        for piece in range(2, len(pieces)):
            load_piece(piece)

        w1_codes = const.tile([P, BRANCHES * S_PASSES, INTER], U32, align_bytes=64)
        w1_planes = const.tile([P, INTER], U8, align_bytes=64)

        def move_w1_planes():
            nc.vector.tensor_copy(
                out=w1_planes[:].rearrange("p (k m) -> p m k", k=PACK), in_=w1_raw_planes[:].rearrange("p (m k) -> p m k", k=PACK)
            )

        def move_w1_codes(n):
            passes = slice(S_PASSES * n, S_PASSES * (n + 1))
            nc.vector.tensor_copy(
                out=w1_codes[:, passes, :].bitcast(I32).rearrange("p c (k m) -> p c k m", k=PACK),
                in_=w1_raw_codes[:, passes, :].bitcast(I32).rearrange("p c (m k) -> p c k m", k=PACK),
            )

        factor = const.tile([P, CH], F32)
        offset = const.tile([P, CH], F32)
        minus_half = const.tile([P, CH], F32)
        nc.gpsimd.memset(minus_half[:], -0.5)
        vec2 = const.tile([P, 5, CH2], F32)
        warm = const.tile([P, 2], F32)
        nc.vector.memset(warm[:], 0.0)
        nc.scalar.activation(out=warm[:, 1:2], in_=warm[:, 0:1], func=ACT.Sigmoid)

        def factor_steps(columns, vectors):
            bias_v, gain_v, beta_v, mean_v, var_v = vectors
            variance = const.tile([P, CH2], F32, name="variance%d" % columns.start)
            cols = slice(0, columns.stop - columns.start)

            def first():
                nc.vector.tensor_scalar_add(variance[:, cols], var_v, EPS)
                nc.gpsimd.tensor_tensor(out=factor[:, columns], in0=variance[:, cols], in1=minus_half[:, columns], op=ALU.pow)

            def second():
                nc.vector.tensor_tensor(out=offset[:, columns], in0=bias_v, in1=mean_v, op=ALU.subtract)

            def third():
                nc.vector.tensor_tensor(out=factor[:, columns], in0=factor[:, columns], in1=gain_v, op=ALU.mult)

            def fourth():
                nc.vector.tensor_tensor(out=offset[:, columns], in0=offset[:, columns], in1=factor[:, columns], op=ALU.mult)

            def fifth():
                nc.vector.tensor_tensor(out=offset[:, columns], in0=offset[:, columns], in1=beta_v, op=ALU.add)

            return first, second, third, fourth, fifth

        def transpose_vectors2():
            vec_ps = flips.tile([P, P], BF16, tag="bank")
            nc.tensor.transpose(vec_ps[:], vec2_rows[:], ident_bf[:])
            return vec_ps

        def copy_vectors2(vec_ps):
            nc.vector.tensor_copy(out=vec2[:], in_=vec_ps[:, 0 : 5 * CH2].rearrange("p (v c) -> p v c", v=5))

        def as_words(tile3):
            return tile3.rearrange("p x y -> p (x y)").bitcast(F32)

        s_rows, s_grouped, s_codes, s_planes = {}, {}, {}, {}
        h_cols, h_groups, h_codes, h_planes = {}, {}, {}, {}
        gate_cols, out_sb, term_sb = {}, {}, {}

        def on_vector(step):
            return step == len(steps) - 1 or False

        def add_branches(piece):
            g, pair = pieces[piece]
            tiles = slice(2 * pair, 2 * pair + 2)
            s_pair = work.tile([P, 2, DIM // 2, 2], BF16)
            for first_tile, last_tile in ((0, 1), (1, 2)) if piece < 1 else ((0, 2),):
                tiles = slice(2 * pair + first_tile, 2 * pair + last_tile)
                words = slice(DIM // 4 * first_tile, DIM // 4 * last_tile)
                terms_in = [
                    t_sb[g][:, n, tiles, :].rearrange("p a d -> p (a d)").rearrange("p (x u e) -> p u x e", u=2, e=2)
                    for n in range(BRANCHES)
                ]
                nc.vector.tensor_tensor(out=s_pair[:, :, words, :], in0=terms_in[0], in1=terms_in[1], op=ALU.add)
            s_rows[piece] = s_pair

        def transpose_sum(piece, a):
            words = s_rows[piece][:].rearrange("p u x e -> p (u x e)").bitcast(F32)
            if a == 0:
                s_grouped[piece] = work.tile([P, S_PASSES, PAIR, PACK], BF16, align_bytes=64, name="s_grouped", tag="s_grouped")
            bank = flips.tile([P, S_PASSES, 2, P], F32, tag="bank")
            for c in range(S_PASSES):
                for u in range(2):
                    first = (DIM // 2) * u + P * (S_PASSES * a + c)
                    nc.tensor.transpose(bank[:, c, u, :], words[:, first : first + P], ident_f[:])
            grouped = s_grouped[piece][:].rearrange("p c r k -> p c (r k)").bitcast(F32).rearrange("p c (r u) -> p c r u", u=2)
            nc.scalar.copy(out=grouped[:, :, P * a : P * (a + 1), :], in_=bank[:].rearrange("p c u r -> p c r u"))

        def quantise_sum(piece):
            s_codes[piece] = operands.tile([P, S_PASSES * PAIR], U32, align_bytes=64, name="s_codes", tag="s_codes")
            s_planes[piece] = operands.tile([P, S_PASSES * PAIR], U8, align_bytes=64, name="s_planes", tag="s_planes")
            nc.vector.quantize_mx(
                out=s_codes[piece][:].bitcast(FP8X4),
                scales=s_planes[piece][:],
                in_=s_grouped[piece][:].rearrange("p s c k -> p (s c k)"),
            )

        def first_layer(unit):
            g, u = units[unit]
            wide = WIDTHS[g] == 4
            cols = P * WIDTHS[g]
            acc = sums.tile([P, 2, PAIR], F32, name="acc", tag="bank")
            if wide:
                n, ks = u // KS, (u % KS,)
            else:
                n, ks = u // 2, (2 * (u % 2), 2 * (u % 2) + 1)
            if u == 0 or (wide and u == KS):
                h_cols[(g, n)] = work.tile([P, KS, 2 * PAIR], BF16, name="h_half", tag="h_half")
                if not wide:
                    h_cols[(g, 1)] = h_cols[(g, 0)]
            for i in range(2):
                k = ks[0] if wide else ks[i]
                channels = slice(P * k, P * (k + 1))
                piece = pieces.index((g, i if wide else 0))
                for c in range(S_PASSES):
                    w = S_PASSES * n + c
                    columns = slice(PAIR * c, PAIR * (c + 1))
                    nc.tensor.matmul_mx(
                        out=acc[:, i, :],
                        lhsT=w1_codes[:, w, channels].bitcast(FP8X4),
                        lhsT_scale=w1_planes[4 * w : P, channels],
                        rhs=s_codes[piece][:, columns].bitcast(FP8X4),
                        rhs_scale=s_planes[piece][:, columns],
                        start=(c == 0),
                        stop=(c == S_PASSES - 1),
                    )
            for i, k in enumerate(ks):
                ch = KS * n + k
                first_col = 0 if wide else PAIR * n
                nc.scalar.activation(
                    out=h_cols[(g, n)][:, k, first_col : first_col + cols],
                    in_=acc[:].rearrange("p i b -> p (i b)") if wide else acc[:, i, :],
                    func=ACT.Relu, bias=offset[:, ch : ch + 1], scale=factor[:, ch : ch + 1],
                )

        def regroup_hidden(quad, part=0, parts=1):
            if part == 0:
                h_groups[quad] = work.tile([P, 2 * PAIR, PACK], BF16, align_bytes=64, name="h_grouped", tag="h_grouped")
            columns = slice(2 * PAIR // parts * part, 2 * PAIR // parts * (part + 1))
            nc.vector.tensor_copy(
                out=h_groups[quad][:, columns, :].rearrange("p (c i) k -> p c k i", i=4),
                in_=h_cols[quads[quad]][:, :, columns].rearrange("p k (c i) -> p c k i", i=4),
            )

        def quantise_hidden(quad, part=0, parts=1):
            if part == 0:
                h_codes[quads[quad]] = operands.tile([P, 2 * PAIR], U32, align_bytes=64, name="h_codes", tag="h_codes")
                h_planes[quads[quad]] = operands.tile([P, 2 * PAIR], U8, align_bytes=64, name="h_planes", tag="h_planes")
            columns = slice(2 * PAIR // parts * part, 2 * PAIR // parts * (part + 1))
            nc.vector.quantize_mx(
                out=h_codes[quads[quad]][:, columns].bitcast(FP8X4),
                scales=h_planes[quads[quad]][:, columns],
                in_=h_groups[quad][:, columns, :].rearrange("p c k -> p (c k)"),
            )

        def second_layer(step):
            g, j0 = steps[step]
            cols = P * WIDTHS[g]
            for i in range(2):
                acc = sums.tile([P, 2 * PAIR], F32, name="acc2", tag="bank")
                gate = gates.tile([P, 2 * PAIR], F32)
                for part in range(1 if WIDTHS[g] == 4 else 2):
                    j, n = (j0, i) if WIDTHS[g] == 4 else (j0 + i, part)
                    features = slice(P * j, P * (j + 1))
                    columns = slice(cols * part, cols * (part + 1))
                    key = (g, n) if WIDTHS[g] == 4 else (g, 0)
                    nc.tensor.matmul_mx(
                        out=acc[:, columns],
                        lhsT=w2_codes[:, n, features].bitcast(FP8X4),
                        lhsT_scale=w2_planes[4 * n : P, features],
                        rhs=h_codes[key][:, columns].bitcast(FP8X4),
                        rhs_scale=h_planes[key][:, columns],
                        start=True,
                        stop=True,
                    )
                for part in range(1 if WIDTHS[g] == 4 else 2):
                    j, n = (j0, i) if WIDTHS[g] == 4 else (j0 + i, part)
                    columns = slice(cols * part, cols * (part + 1))
                    ch = CH1 + D_TILES * n + j
                    nc.scalar.activation(
                        out=gate[:, columns], in_=acc[:, columns], func=ACT.Sigmoid,
                        bias=offset[:, ch : ch + 1], scale=factor[:, ch : ch + 1],
                    )
                gate_cols[(step, i)] = gate

        def apply_gates(step):
            g, j0 = steps[step]
            wide = WIDTHS[g] == 4
            if j0 == 0:
                out_sb[g] = work.tile([P, 4, DIM], F32, name="out_sb", tag="out_sb")
            term = terms.tile([P, 2, 4, P], F32, name="term", tag="term")
            for i in range(2):
                bank = flips.tile([P, 4, P], F32, tag="bank")
                for a in range(4):
                    nc.tensor.transpose(bank[:, a, :], gate_cols[(step, i)][:, P * a : P * (a + 1)], ident_f[:])
                if wide:
                    t_in = t_sb[g][:, i, :, P * j0 : P * (j0 + 1)]
                else:
                    t_in = t_sb[g][:].rearrange("p n a d -> p (n a) d")[:, :, P * (j0 + i) : P * (j0 + i + 1)]
                nc.vector.scalar_tensor_tensor(
                    out=term[:, i], in0=t_in, scalar=3.0, in1=bank[:], op0=ALU.mult, op1=ALU.mult
                )
            term_sb[step] = term

        def add_terms(step):
            g, j0 = steps[step]
            wide = WIDTHS[g] == 4
            term = term_sb[step]
            adder = nc.vector if on_vector(step) else nc.gpsimd
            if wide:
                adder.tensor_tensor(out=out_sb[g][:, :, P * j0 : P * (j0 + 1)], in0=term[:, 0], in1=term[:, 1], op=ALU.add)
            else:
                out_tiles = out_sb[g][:, 0:2, P * j0 : P * (j0 + 2)].rearrange("p a (i d) -> p i a d", i=2)
                for tiles in (slice(0, 1), slice(1, 2)) if step == len(steps) - 1 else (slice(0, 2),):
                    adder.tensor_tensor(out=out_tiles[:, tiles], in0=term[:, tiles, 0:2], in1=term[:, tiles, 2:4], op=ALU.add)

        def store(step):
            g, j0 = steps[step]
            if step == len(steps) - 1:
                for j in (j0, j0 + 1):
                    done = slice(P * j, P * (j + 1))
                    nc.sync.dma_start(out=out_rows[g][:, :, done], in_=out_sb[g][:, 0 : WIDTHS[g], done])
                return
            elif step == len(steps) - 2:
                done = slice(P * (j0 - (j0 % 2)), P * (j0 + 1)) if WIDTHS[g] == 4 else slice(P * j0, P * (j0 + 2))
            elif WIDTHS[g] == 4:
                if j0 % 2 == 0:
                    return
                done = slice(P * (j0 - 1), P * (j0 + 1))
            else:
                done = slice(P * j0, P * (j0 + 2))
            nc.sync.dma_start(out=out_rows[g][:, :, done], in_=out_sb[g][:, 0 : WIDTHS[g], done])

        units = [(g, u) for g in range(GROUPS) for u in range(2 * WIDTHS[g])]
        steps = [(g, j) for g in range(GROUPS) for j in range(0, D_TILES, 4 // WIDTHS[g])]
        quads = []
        for g in range(GROUPS):
            quads += [(g, 0), (g, 1)] if WIDTHS[g] == 4 else [(g, 0)]
        QUADS = len(quads)

        dummy = const.tile([P, 512], BF16)
        nc.vector.memset(dummy[:], 0.0)
        warm_ps = sums.tile([P, 512], F32, name="warm_ps", tag="bank")

        def warm_up(count):
            for dummy_pass in range(count):
                nc.tensor.matmul(warm_ps[:], lhsT=ident_bf[:], rhs=dummy[:], start=True, stop=True)

        factors1 = factor_steps(slice(0, CH1), [vec1_bf[:, v, 0:CH1] for v in range(5)])
        factors2 = factor_steps(slice(CH1, CH), [vec2[:, v, :] for v in range(5)])
        add_branches(0)
        warm_up(4)
        transpose_sum(0, 0)
        transpose_sum(0, 1)
        warm_up(2)
        vectors2 = transpose_vectors2()
        factors1[0]()
        move_w1_planes()
        factors1[1]()
        move_w1_codes(0)
        quantise_sum(0)
        factors1[2]()
        copy_vectors2(vectors2)
        factors1[3]()
        factors2[0]()
        factors1[4]()
        first_layer(0)
        first_layer(1)
        move_w1_codes(1)
        first_layer(2)
        first_layer(3)
        factors2[1]()
        add_branches(1)
        regroup_hidden(0, 0, 2)
        transpose_sum(1, 0)
        transpose_sum(1, 1)
        warm_ps = sums.tile([P, 512], F32, name="warm_ps", tag="bank")
        warm_up(2)
        regroup_hidden(0, 1, 2)
        factors2[2]()
        quantise_hidden(0, 0, 2)
        factors2[3]()
        quantise_hidden(0, 1, 2)
        factors2[4]()
        quantise_sum(1)

        unit_steps = [0, 0, 1, 1, 3, 3, 4, 4, 5, 6, 7, 8] + [4 * q - 7 + u for q in range(4, 8) for u in range(4)]
        add_step = {2: 0, 3: 1, 4: 4, 5: 7, 6: 11, 7: 15}
        qs_step = {2: 2, 3: 3, 4: 8, 5: 12, 6: 16, 7: 20}
        rg_step = {q: unit_steps[4 * (q - 1) + 3] + 1 for q in range(1, len(quads))}
        for step in range(len(steps) + 1):
            def vector_work():
                if step > 1 and on_vector(step - 2):
                    add_terms(step - 2)
                    store(step - 2)
                for q in rg_step:
                    if rg_step[q] + 1 == step:
                        quantise_hidden(q)
                for q in rg_step:
                    if rg_step[q] == step:
                        regroup_hidden(q)
                for piece in add_step:
                    if qs_step[piece] == step:
                        quantise_sum(piece)
                for piece in add_step:
                    if add_step[piece] == step:
                        add_branches(piece)

            def layer1():
                for i in range(len(unit_steps)):
                    if unit_steps[i] == step:
                        first_layer(4 + i)

            def flips_s():
                for piece in add_step:
                    for c in range(2):
                        if step == add_step[piece] + (1, 1)[c]:
                            transpose_sum(piece, c)
            def layer2():
                if step < len(steps):
                    second_layer(step)
            def gates_():
                if step > 0:
                    apply_gates(step - 1)
                    if not on_vector(step - 1) or step == len(steps):
                        add_terms(step - 1)
                        store(step - 1)
            vector_work()
            layer2()
            layer1()
            gates_()
            flips_s()
